import numpy as np
import ml_dtypes

BF16 = ml_dtypes.bfloat16


def bf(x):
    return np.asarray(x, np.float32).astype(BF16)


def f32(x):
    return np.asarray(x, np.float32)


def f64(x):
    return np.asarray(x).astype(np.float64)


def striped(idx):
    return np.tile(idx.reshape(-1, 16).T, (8, 1))


C, S, N, K, H, B, Q = 512, 2048, 2048, 256, 4, 2, 3
DH, T = C // H, N // K
A_QKV, A_PROJ, A_BIAS = 1.25, 2.0, 0.1


def setup_inputs():
    return {
        "feat": f32(np.random.standard_normal((C, S))),
        "cls_tok": bf(np.random.standard_normal((C, B))),
        "wqkv": bf(A_QKV * np.random.standard_normal((C, Q * C)) / np.sqrt(C)),
        "bqkv": f32(A_BIAS * np.random.standard_normal((Q * C, 1))),
        "wproj": bf(A_PROJ * np.random.standard_normal((C, C)) / np.sqrt(C)),
        "bproj": f32(A_BIAS * np.random.standard_normal((C, 1))),
        "offs": striped(np.random.permutation(S)[:N]),
    }


def reference(feat, cls_tok, wqkv, bqkv, wproj, bproj, offs):
    idx = offs[:16].T.reshape(-1)
    p = f64(wqkv).T @ f64(feat)
    qkv = (p[:, idx] + f64(bqkv)).reshape(Q, H, DH, T, K)
    cq = (f64(wqkv).T @ f64(cls_tok) + f64(bqkv)).reshape(Q, H, DH, B)
    cq = np.repeat(cq, T // B, axis=-1)[..., None]
    q = qkv[0]
    kk = np.concatenate([cq[1], qkv[1]], axis=-1)
    vv = np.concatenate([cq[2], qkv[2]], axis=-1)
    e = np.einsum("hdta,hdti->htai", q, kk, optimize=True) * DH ** -0.5
    w = np.exp(e - e.max(axis=-1, keepdims=True))
    w = w / w.sum(axis=-1, keepdims=True)
    att = np.einsum("htai,hdti->hdta", w, vv, optimize=True).reshape(C, N)
    return f64(wproj).T @ att + f64(bproj)

@@ -1,0 +1,318 @@
+from contextlib import ExitStack
+
+import concourse.mybir as mybir
+from concourse.masks import make_identity
+
+F32 = mybir.dt.float32
+BF16 = mybir.dt.bfloat16
+U16 = mybir.dt.uint16
+ADD = mybir.AluOpType.add
+MULT = mybir.AluOpType.mult
+EXP = mybir.ActivationFunctionType.Exp
+IDENTITY = mybir.ActivationFunctionType.Identity
+ALONG_FREE = mybir.AxisListType.X
+
+PART = 128
+C = 512
+POINTS = 2048
+HEADS = 4
+DH = C // HEADS
+PATCH = 256
+PATCHES = POINTS // PATCH
+CLOUDS = 2
+PATCHES_PER_CLOUD = PATCHES // CLOUDS
+KEYS = PATCH + 1
+KEY_PITCH = 264
+C_BLOCKS = C // PART
+ROW_BLOCKS = 3 * C // PART
+CHUNK = 512
+CHUNKS = POINTS // CHUNK
+PAIR = CHUNK // PATCH
+HALVES = PATCH // PART
+OFFSET_COLS = PATCH // 16
+SCALE = DH**-0.5
+
+FLOPS = (
+    2 * C * 3 * C * POINTS
+    + 2 * C * 2 * C * CLOUDS
+    + 2 * 2 * HEADS * PATCHES * DH * PATCH * KEYS
+    + 2 * C * C * POINTS
+)
+
+
+def tile_serializedattention_b_kernel(tc, feat, cls_tok, wqkv, bqkv, wproj, bproj, offs, out):
+    nc = tc.nc
+    with ExitStack() as ctx:
+        held = ctx.enter_context(tc.tile_pool(name="held", bufs=1))
+        stage = ctx.enter_context(tc.tile_pool(name="stage", bufs=2))
+        windows = ctx.enter_context(tc.tile_pool(name="windows", bufs=2))
+        picks = ctx.enter_context(tc.tile_pool(name="picks", bufs=2))
+        per_head = ctx.enter_context(tc.tile_pool(name="per_head", bufs=3))
+        stats = ctx.enter_context(tc.tile_pool(name="stats", bufs=6))
+        exps = ctx.enter_context(tc.tile_pool(name="exps", bufs=4))
+        per_pair = ctx.enter_context(tc.tile_pool(name="per_pair", bufs=3))
+        per_patch = ctx.enter_context(tc.tile_pool(name="per_patch", bufs=2))
+        results = ctx.enter_context(tc.tile_pool(name="results", bufs=3))
+        sums = ctx.enter_context(tc.psum_pool(name="sums", bufs=2))
+        logits = ctx.enter_context(tc.psum_pool(name="logits", bufs=4))
+        flips = ctx.enter_context(tc.psum_pool(name="flips", bufs=2))
+
+        zero = held.tile([PART, 1], F32, name="zero")
+        nc.vector.memset(zero[:], 0.0)
+        one = held.tile([PART, 1], F32, name="one")
+        nc.scalar.activation(out=one[:], in_=zero[:], func=EXP)
+
+        offsets = held.tile([PART, POINTS // 16], U16, name="offsets")
+        wqkv_sb = held.tile([PART, C_BLOCKS, 3 * C], BF16, name="wqkv_sb")
+        wqkv_blocks = wqkv.rearrange("(cb p) r -> p cb r", p=PART)
+        wproj_sb = held.tile([PART, C_BLOCKS, C], BF16, name="wproj_sb")
+        feat_bf = held.tile([PART, C_BLOCKS, POINTS], BF16, name="feat_bf")
+        feat_blocks = feat.rearrange("(cb p) s -> p cb s", p=PART)
+        cls_sb = held.tile([PART, C_BLOCKS, CLOUDS], BF16, name="cls_sb")
+        bias_rows = held.tile([PART, PART], F32, name="bias_rows")
+        nc.vector.memset(bias_rows[:], 0.0)
+
+        nc.gpsimd.dma_start(wqkv_sb[:, :, 0:C], wqkv_blocks[:, :, 0:C])
+        for n in range(CHUNKS):
+            cols = slice(n * CHUNK, (n + 1) * CHUNK)
+            low = stage.tile([PART, 2, CHUNK], F32, name="low")
+            nc.sync.dma_start(low[:], feat_blocks[:, 0:2, cols])
+            nc.vector.tensor_copy(feat_bf[:, 0:2, cols], low[:])
+            high = stage.tile([PART, 2, CHUNK], F32, name="high")
+            nc.scalar.dma_start(high[:], feat_blocks[:, 2:4, cols])
+            nc.scalar.copy(feat_bf[:, 2:4, cols], high[:])
+            if n == 0:
+                nc.sync.dma_start(offsets[:], offs)
+                nc.gpsimd.dma_start(bias_rows[0:ROW_BLOCKS, :], bqkv.rearrange("(b p) o -> b (p o)", p=PART))
+                nc.gpsimd.dma_start(
+                    bias_rows[ROW_BLOCKS : ROW_BLOCKS + C_BLOCKS, :], bproj.rearrange("(b p) o -> b (p o)", p=PART)
+                )
+                nc.gpsimd.dma_start(cls_sb[:], cls_tok.rearrange("(cb p) u -> p cb u", p=PART))
+        nc.sync.dma_start(wqkv_sb[:, :, C : 2 * C], wqkv_blocks[:, :, C : 2 * C])
+        nc.scalar.dma_start(wqkv_sb[:, :, 2 * C : 3 * C], wqkv_blocks[:, :, 2 * C : 3 * C])
+        nc.sync.dma_start(wproj_sb[:], wproj.rearrange("(cb p) m -> p cb m", p=PART))
+
+        ident_f32 = held.tile([PART, PART], F32, name="ident_f32")
+        make_identity(nc, ident_f32[:])
+        ident = held.tile([PART, PART], BF16, name="ident")
+        make_identity(nc, ident[:])
+
+        bias_ps = sums.tile([PART, CHUNK], F32, name="bias_ps", tag="sum_ps")
+        nc.tensor.transpose(bias_ps[:, 0:PART], bias_rows[:], ident_f32[:])
+        bias = held.tile([PART, ROW_BLOCKS + C_BLOCKS], F32, name="bias")
+        nc.vector.tensor_copy(bias[:], bias_ps[:, 0 : ROW_BLOCKS + C_BLOCKS])
+        bias_wide = held.tile([PART, ROW_BLOCKS, PATCH], F32, name="bias_wide")
+        nc.gpsimd.tensor_copy(
+            bias_wide[:], bias[:, 0:ROW_BLOCKS].unsqueeze(2).to_broadcast([PART, ROW_BLOCKS, PATCH])
+        )
+
+        value_windows = [held.tile([PART, POINTS], F32, name=f"value_window{h}") for h in range(HEADS)]
+        wT = held.tile([PART, HEADS, PATCHES, HALVES, PATCH], BF16, name="wT")
+        cls_w = held.tile([PART, PATCHES, HALVES, PART], BF16, name="cls_w")
+        nc.gpsimd.memset(cls_w[:], 0.0)
+        att_bf = held.tile([PART, HEADS, POINTS], BF16, name="att_bf")
+
+        def project_chunk(r, n, window):
+            cols = slice(n * CHUNK, (n + 1) * CHUNK)
+            p_ps = sums.tile([PART, CHUNK], F32, name="p_ps", tag="sum_ps")
+            for cb in range(C_BLOCKS):
+                nc.tensor.matmul(
+                    p_ps[:],
+                    lhsT=wqkv_sb[:, cb, r * PART : (r + 1) * PART],
+                    rhs=feat_bf[:, cb, cols],
+                    start=(cb == 0),
+                    stop=(cb == C_BLOCKS - 1),
+                )
+            nc.scalar.copy(window[:, cols], p_ps[:])
+
+        def look_up(picked, r, window, t):
+            piece = offsets[:, t * OFFSET_COLS : (t + 1) * OFFSET_COLS]
+            nc.vector.tensor_tensor(picked, window[:].indirect(piece), bias_wide[:, r, :], ADD)
+
+        def look_up_rows(r, window, rounded):
+            for u in range(CLOUDS):
+                picked = picks.tile([PART, PATCHES_PER_CLOUD, PATCH], F32, name="picked")
+                for i in range(PATCHES_PER_CLOUD):
+                    look_up(picked[:, i, :], r, window, u * PATCHES_PER_CLOUD + i)
+                nc.gpsimd.tensor_copy(
+                    rounded[:, u * PATCHES_PER_CLOUD : (u + 1) * PATCHES_PER_CLOUD, 0:PATCH], picked[:]
+                )
+
+        def project_class_tokens(r):
+            cq_ps = logits.tile([PART, KEYS], F32, name="cq_ps", tag="e_ps")
+            for cb in range(C_BLOCKS):
+                nc.tensor.matmul(
+                    cq_ps[:, 0:CLOUDS],
+                    lhsT=wqkv_sb[:, cb, r * PART : (r + 1) * PART],
+                    rhs=cls_sb[:, cb, :],
+                    start=(cb == 0),
+                    stop=(cb == C_BLOCKS - 1),
+                )
+            return cq_ps
+
+        def softmax_weights(h, q_bf, k_bf, pair):
+            w = per_pair.tile([PART, PAIR, HALVES, KEY_PITCH], BF16, name="w")
+            for i in range(PAIR):
+                t = pair * PAIR + i
+                top = stats.tile([PART, HALVES], F32, name="top")
+                shift = stats.tile([PART, HALVES], F32, name="shift")
+                total = stats.tile([PART, HALVES], F32, name="total")
+                recip = stats.tile([PART, HALVES], F32, name="recip")
+                e_tiles = []
+                for jb in range(HALVES):
+                    e_ps = logits.tile([PART, KEYS], F32, name="e_ps")
+                    nc.tensor.matmul(
+                        e_ps[:],
+                        lhsT=q_bf[:, t, jb * PART : (jb + 1) * PART],
+                        rhs=k_bf[:, t, 0:KEYS],
+                        start=True,
+                        stop=True,
+                    )
+                    nc.vector.reduce_max(out=top[:, jb : jb + 1], in_=e_ps[:], axis=ALONG_FREE)
+                    e_tiles.append(e_ps)
+                nc.vector.tensor_scalar(out=shift[:], in0=top[:], scalar1=-SCALE, scalar2=None, op0=MULT)
+                ex_tiles = []
+                for jb in range(HALVES):
+                    ex = exps.tile([PART, KEYS], F32, name="ex")
+                    nc.scalar.activation(
+                        out=ex[:],
+                        in_=e_tiles[jb][:],
+                        func=EXP,
+                        bias=shift[:, jb : jb + 1],
+                        scale=SCALE,
+                        accum_out=total[:, jb : jb + 1],
+                    )
+                    ex_tiles.append(ex)
+                nc.vector.reciprocal(recip[:], total[:])
+                for jb in range(HALVES):
+                    nc.gpsimd.tensor_scalar(
+                        out=w[:, i, jb, 0:KEYS],
+                        in0=ex_tiles[jb][:],
+                        scalar1=recip[:, jb : jb + 1],
+                        scalar2=1.0,
+                        op0=MULT,
+                        op1=MULT,
+                    )
+            patches = slice(pair * PAIR, (pair + 1) * PAIR)
+            nc.gpsimd.tensor_copy(cls_w[:, patches, :, h], w[:, :, :, PATCH])
+            wT_ps = flips.tile([PART, PAIR, HALVES, PATCH], BF16, name="wT_ps", tag="flip_ps")
+            for i in range(PAIR):
+                for ib in range(HALVES):
+                    for jb in range(HALVES):
+                        nc.tensor.transpose(
+                            wT_ps[:, i, ib, jb * PART : (jb + 1) * PART],
+                            w[:, i, jb, ib * PART : (ib + 1) * PART],
+                            ident[:],
+                        )
+            nc.scalar.copy(wT[:, h, patches, :, :], wT_ps[:])
+
+        def flip_class_weights(pair):
+            cls_wT_ps = flips.tile([PART, PAIR, PATCH], BF16, name="cls_wT_ps", tag="flip_ps")
+            for i in range(PAIR):
+                for jb in range(HALVES):
+                    nc.tensor.transpose(
+                        cls_wT_ps[:, i, jb * PART : (jb + 1) * PART], cls_w[:, pair * PAIR + i, jb, :], ident[:]
+                    )
+            cls_wT = per_pair.tile([PART, PAIR, PATCH], BF16, name="cls_wT")
+            nc.scalar.copy(cls_wT[:], cls_wT_ps[:])
+            return cls_wT
+
+        def attend(t, cls_wT_t):
+            u = t // PATCHES_PER_CLOUD
+            picked_v = per_patch.tile([PART, HEADS, PATCH], F32, name="picked_v")
+            for h in range(HEADS):
+                look_up(picked_v[:, h, :], 2 * HEADS + h, value_windows[h], t)
+            v_bf = per_patch.tile([PART, HEADS, PATCH], BF16, name="v_bf")
+            nc.gpsimd.tensor_copy(v_bf[:], picked_v[:])
+            vT_ps = flips.tile([PART, HALVES, HEADS, DH], BF16, name="vT_ps", tag="flip_ps")
+            for h in range(HEADS):
+                for ib in range(HALVES):
+                    nc.tensor.transpose(vT_ps[:, ib, h, :], v_bf[:, h, ib * PART : (ib + 1) * PART], ident[:])
+            vT = per_patch.tile([PART, HALVES, HEADS, DH], BF16, name="vT")
+            nc.scalar.copy(vT[:], vT_ps[:])
+            for first in range(0, HEADS, 2):
+                att_ps = logits.tile([PART, 2, PATCH], F32, name="att_ps", tag="e_ps")
+                for i in range(2):
+                    h = first + i
+                    for ib in range(HALVES):
+                        nc.tensor.matmul(
+                            att_ps[:, i, :], lhsT=vT[:, ib, h, :], rhs=wT[:, h, t, ib, :], start=(ib == 0), stop=False
+                        )
+                    nc.tensor.matmul(att_ps[:, i, :], lhsT=cv_rows[:, u, h, :], rhs=cls_wT_t, start=False, stop=True)
+                nc.scalar.copy(att_bf[:, first : first + 2, t * PATCH : (t + 1) * PATCH], att_ps[:])
+
+        def project_out(n):
+            cols = slice(n * CHUNK, (n + 1) * CHUNK)
+            for m in range(C_BLOCKS):
+                out_ps = sums.tile([PART, CHUNK], F32, name="out_ps", tag="sum_ps")
+                for h in range(HEADS):
+                    nc.tensor.matmul(
+                        out_ps[:],
+                        lhsT=wproj_sb[:, h, m * PART : (m + 1) * PART],
+                        rhs=att_bf[:, h, cols],
+                        start=(h == 0),
+                        stop=(h == HEADS - 1),
+                    )
+                out_sb = results.tile([PART, CHUNK], F32, name="out_sb")
+                nc.scalar.activation(
+                    out=out_sb[:], in_=out_ps[:], func=IDENTITY, bias=bias[:, ROW_BLOCKS + m : ROW_BLOCKS + m + 1]
+                )
+                nc.sync.dma_start(out[m * PART : (m + 1) * PART, cols], out_sb[:])
+
+        q_of = {}
+        k_of = {}
+        for h in range(HEADS):
+            q_of[h] = per_head.tile([PART, PATCHES, PATCH], BF16, name="q_bf")
+            k_of[h] = per_head.tile([PART, PATCHES, KEY_PITCH], BF16, name="k_bf")
+            q_window = windows.tile([PART, POINTS], F32, name="q_window", tag="window")
+            k_window = windows.tile([PART, POINTS], F32, name="k_window", tag="window")
+            blocks = ((h, q_window, q_of[h]), (HEADS + h, k_window, k_of[h]), (2 * HEADS + h, value_windows[h], None))
+            if h == 0:
+                jobs = [(b, n) for n in range(CHUNKS) for b in (0, 1)] + [(2, n) for n in range(CHUNKS)]
+            else:
+                jobs = [(b, n) for b in range(3) for n in range(CHUNKS)]
+            share = len(jobs) // CHUNKS
+            for pair in range(CHUNKS):
+                if h > 0:
+                    softmax_weights(h - 1, q_of[h - 1], k_of[h - 1], pair)
+                for b, n in jobs[pair * share : (pair + 1) * share]:
+                    r, window, rounded = blocks[b]
+                    project_chunk(r, n, window)
+                    if n == CHUNKS - 1 and rounded is not None:
+                        look_up_rows(r, window, rounded)
+
+            if h == 0:
+                ck = held.tile([PART, HEADS, CLOUDS], F32, name="ck")
+                for g in range(HEADS):
+                    r = HEADS + g
+                    cq_ps = project_class_tokens(r)
+                    nc.vector.tensor_scalar(
+                        out=ck[:, g, :], in0=cq_ps[:, 0:CLOUDS], scalar1=bias[:, r : r + 1], scalar2=None, op0=ADD
+                    )
+                cv_cols = held.tile([PART, CLOUDS, HEADS, PART], BF16, name="cv_cols")
+                nc.gpsimd.memset(cv_cols[:], 0.0)
+                for g in range(HEADS):
+                    r = 2 * HEADS + g
+                    cq_ps = project_class_tokens(r)
+                    nc.vector.tensor_scalar(
+                        out=cv_cols[:, :, g, g], in0=cq_ps[:, 0:CLOUDS], scalar1=bias[:, r : r + 1], scalar2=None, op0=ADD
+                    )
+                cv_ps = flips.tile([PART, CLOUDS, HEADS, DH], BF16, name="cv_ps", tag="flip_ps")
+                for u in range(CLOUDS):
+                    for g in range(HEADS):
+                        nc.tensor.transpose(cv_ps[:, u, g, :], cv_cols[:, u, g, :], ident[:])
+                cv_rows = held.tile([PART, CLOUDS, HEADS, DH], BF16, name="cv_rows")
+                nc.vector.tensor_copy(cv_rows[:], cv_ps[:])
+
+            nc.gpsimd.tensor_copy(
+                k_of[h][:, :, PATCH:KEYS].rearrange("p (u t) o -> p u (t o)", u=CLOUDS),
+                ck[:, h, :].unsqueeze(2).to_broadcast([PART, CLOUDS, PATCHES_PER_CLOUD]),
+            )
+
+        last = HEADS - 1
+        for pair in range(CHUNKS):
+            softmax_weights(last, q_of[last], k_of[last], pair)
+            cls_wT = flip_class_weights(pair)
+            for i in range(PAIR):
+                attend(pair * PAIR + i, cls_wT[:, i, :])
+            project_out(pair)

@@ -27,10 +27,12 @@ C_BLOCKS = C // PART
 ROW_BLOCKS = 3 * C // PART
 CHUNK = 512
 CHUNKS = POINTS // CHUNK
-PAIR = CHUNK // PATCH
+SLICE = CHUNK // 2
+STAGED = 4
 HALVES = PATCH // PART
 OFFSET_COLS = PATCH // 16
 SCALE = DH**-0.5
+EARLY_HEADS = 2
 
 FLOPS = (
     2 * C * 3 * C * POINTS
@@ -44,23 +46,18 @@ def tile_serializedattention_b_kernel(tc, feat, cls_tok, wqkv, bqkv, wproj, bpro
     nc = tc.nc
     with ExitStack() as ctx:
         held = ctx.enter_context(tc.tile_pool(name="held", bufs=1))
-        stage = ctx.enter_context(tc.tile_pool(name="stage", bufs=2))
-        windows = ctx.enter_context(tc.tile_pool(name="windows", bufs=2))
-        picks = ctx.enter_context(tc.tile_pool(name="picks", bufs=2))
+        stage = ctx.enter_context(tc.tile_pool(name="stage", bufs=STAGED))
+        windows = ctx.enter_context(tc.tile_pool(name="windows", bufs=6))
+        picks = ctx.enter_context(tc.tile_pool(name="picks", bufs=3))
         per_head = ctx.enter_context(tc.tile_pool(name="per_head", bufs=3))
-        stats = ctx.enter_context(tc.tile_pool(name="stats", bufs=6))
-        exps = ctx.enter_context(tc.tile_pool(name="exps", bufs=4))
+        stats = ctx.enter_context(tc.tile_pool(name="stats", bufs=4))
+        exps = ctx.enter_context(tc.tile_pool(name="exps", bufs=6))
         per_pair = ctx.enter_context(tc.tile_pool(name="per_pair", bufs=3))
-        per_patch = ctx.enter_context(tc.tile_pool(name="per_patch", bufs=2))
+        per_patch = ctx.enter_context(tc.tile_pool(name="per_patch", bufs=3))
         results = ctx.enter_context(tc.tile_pool(name="results", bufs=3))
         sums = ctx.enter_context(tc.psum_pool(name="sums", bufs=2))
-        logits = ctx.enter_context(tc.psum_pool(name="logits", bufs=4))
+        logit_banks = ctx.enter_context(tc.psum_pool(name="logit_banks", bufs=4))
         flips = ctx.enter_context(tc.psum_pool(name="flips", bufs=2))
-
-        zero = held.tile([PART, 1], F32, name="zero")
-        nc.vector.memset(zero[:], 0.0)
-        one = held.tile([PART, 1], F32, name="one")
-        nc.scalar.activation(out=one[:], in_=zero[:], func=EXP)
 
         offsets = held.tile([PART, POINTS // 16], U16, name="offsets")
         wqkv_sb = held.tile([PART, C_BLOCKS, 3 * C], BF16, name="wqkv_sb")
@@ -71,26 +68,29 @@ def tile_serializedattention_b_kernel(tc, feat, cls_tok, wqkv, bqkv, wproj, bpro
         cls_sb = held.tile([PART, C_BLOCKS, CLOUDS], BF16, name="cls_sb")
         bias_rows = held.tile([PART, PART], F32, name="bias_rows")
         nc.vector.memset(bias_rows[:], 0.0)
+        staged_of = {}
 
-        nc.gpsimd.dma_start(wqkv_sb[:, :, 0:C], wqkv_blocks[:, :, 0:C])
-        for n in range(CHUNKS):
-            cols = slice(n * CHUNK, (n + 1) * CHUNK)
-            low = stage.tile([PART, 2, CHUNK], F32, name="low")
-            nc.sync.dma_start(low[:], feat_blocks[:, 0:2, cols])
-            nc.vector.tensor_copy(feat_bf[:, 0:2, cols], low[:])
-            high = stage.tile([PART, 2, CHUNK], F32, name="high")
-            nc.scalar.dma_start(high[:], feat_blocks[:, 2:4, cols])
-            nc.scalar.copy(feat_bf[:, 2:4, cols], high[:])
-            if n == 0:
-                nc.sync.dma_start(offsets[:], offs)
-                nc.gpsimd.dma_start(bias_rows[0:ROW_BLOCKS, :], bqkv.rearrange("(b p) o -> b (p o)", p=PART))
-                nc.gpsimd.dma_start(
-                    bias_rows[ROW_BLOCKS : ROW_BLOCKS + C_BLOCKS, :], bproj.rearrange("(b p) o -> b (p o)", p=PART)
-                )
-                nc.gpsimd.dma_start(cls_sb[:], cls_tok.rearrange("(cb p) u -> p cb u", p=PART))
-        nc.sync.dma_start(wqkv_sb[:, :, C : 2 * C], wqkv_blocks[:, :, C : 2 * C])
-        nc.scalar.dma_start(wqkv_sb[:, :, 2 * C : 3 * C], wqkv_blocks[:, :, 2 * C : 3 * C])
-        nc.sync.dma_start(wproj_sb[:], wproj.rearrange("(cb p) m -> p cb m", p=PART))
+        def load_slice(s):
+            staged_of[s] = stage.tile([PART, C_BLOCKS, SLICE], F32, name="staged")
+            nc.sync.dma_start(staged_of[s][:], feat_blocks[:, :, s * SLICE : (s + 1) * SLICE])
+
+        def round_slice(s):
+            nc.vector.tensor_copy(feat_bf[:, :, s * SLICE : (s + 1) * SLICE], staged_of[s][:])
+
+        nc.scalar.dma_start(bias_rows[0:ROW_BLOCKS, :], bqkv.rearrange("(b p) o -> b (p o)", p=PART))
+        nc.scalar.dma_start(
+            bias_rows[ROW_BLOCKS : ROW_BLOCKS + C_BLOCKS, :], bproj.rearrange("(b p) o -> b (p o)", p=PART)
+        )
+        nc.scalar.dma_start(cls_sb[:], cls_tok.rearrange("(cb p) u -> p cb u", p=PART))
+        nc.sync.dma_start(wqkv_sb[:, :, 0 : 2 * C], wqkv_blocks[:, :, 0 : 2 * C])
+        for s in range(STAGED):
+            load_slice(s)
+        nc.sync.dma_start(offsets[:], offs)
+
+        zero = held.tile([PART, 1], F32, name="zero")
+        nc.vector.memset(zero[:], 0.0)
+        one = held.tile([PART, 1], F32, name="one")
+        nc.scalar.activation(out=one[:], in_=zero[:], func=EXP)
 
         ident_f32 = held.tile([PART, PART], F32, name="ident_f32")
         make_identity(nc, ident_f32[:])
@@ -106,13 +106,43 @@ def tile_serializedattention_b_kernel(tc, feat, cls_tok, wqkv, bqkv, wproj, bpro
             bias_wide[:], bias[:, 0:ROW_BLOCKS].unsqueeze(2).to_broadcast([PART, ROW_BLOCKS, PATCH])
         )
 
-        value_windows = [held.tile([PART, POINTS], F32, name=f"value_window{h}") for h in range(HEADS)]
-        wT = held.tile([PART, HEADS, PATCHES, HALVES, PATCH], BF16, name="wT")
+        units = [(h, t) for h in range(EARLY_HEADS) for t in range(PATCHES)] + [
+            (h, t) for t in range(PATCHES) for h in range(EARLY_HEADS, HEADS)
+        ]
+        unit_of = {unit: i for i, unit in enumerate(units)}
+        patch_ending_at = {unit_of[(HEADS - 1, t)]: t for t in range(PATCHES)}
+
+        row_order = [r for h in range(HEADS) for r in (h, HEADS + h)] + [2 * HEADS + h for h in range(HEADS)]
+        projections = [(r, n) for n in range(CHUNKS) for r in row_order[0:2]] + [
+            (r, n) for r in row_order[2:] for n in range(CHUNKS)
+        ]
+        batches = [
+            [(r, u * PATCHES_PER_CLOUD + i) for i in range(PATCHES_PER_CLOUD)]
+            for h in range(HEADS)
+            for u in range(CLOUDS)
+            for r in (h, HEADS + h)
+        ] + [[(2 * HEADS + h, t) for h in range(HEADS)] for t in range(PATCHES)]
+        pieces = [(b, slot) for b in range(len(batches)) for slot in range(len(batches[b]))]
+
+        wT = held.tile([PART, len(units), HALVES, PATCH], BF16, name="wT")
         cls_w = held.tile([PART, PATCHES, HALVES, PART], BF16, name="cls_w")
         nc.gpsimd.memset(cls_w[:], 0.0)
+        cv_cols = held.tile([PART, CLOUDS, HEADS, PART], BF16, name="cv_cols")
+        nc.gpsimd.memset(cv_cols[:], 0.0)
+        cv_rows = held.tile([PART, CLOUDS, HEADS, DH], BF16, name="cv_rows")
+        cq = held.tile([PART, 2 * HEADS, CLOUDS], F32, name="cq")
         att_bf = held.tile([PART, HEADS, POINTS], BF16, name="att_bf")
 
-        def project_chunk(r, n, window):
+        window_of = {}
+        rounded_of = {}
+        picked_of = {}
+        v_of, vT_of, cls_wT_of = {}, {}, {}
+        e_of, shift_of, ex_of, total_of, recip_of = {}, {}, {}, {}, {}
+        w_of = {}
+
+        def project_chunk(r, n):
+            if n == 0:
+                window_of[r] = windows.tile([PART, POINTS], F32, name="window")
             cols = slice(n * CHUNK, (n + 1) * CHUNK)
             p_ps = sums.tile([PART, CHUNK], F32, name="p_ps", tag="sum_ps")
             for cb in range(C_BLOCKS):
@@ -123,196 +153,223 @@ def tile_serializedattention_b_kernel(tc, feat, cls_tok, wqkv, bqkv, wproj, bpro
                     start=(cb == 0),
                     stop=(cb == C_BLOCKS - 1),
                 )
-            nc.scalar.copy(window[:, cols], p_ps[:])
+            nc.scalar.copy(window_of[r][:, cols], p_ps[:])
 
-        def look_up(picked, r, window, t):
-            piece = offsets[:, t * OFFSET_COLS : (t + 1) * OFFSET_COLS]
-            nc.vector.tensor_tensor(picked, window[:].indirect(piece), bias_wide[:, r, :], ADD)
-
-        def look_up_rows(r, window, rounded):
-            for u in range(CLOUDS):
-                picked = picks.tile([PART, PATCHES_PER_CLOUD, PATCH], F32, name="picked")
-                for i in range(PATCHES_PER_CLOUD):
-                    look_up(picked[:, i, :], r, window, u * PATCHES_PER_CLOUD + i)
+        def look_up(b, slot):
+            if slot == 0:
+                picked_of[b] = picks.tile([PART, len(batches[b]), PATCH], F32, name="picked")
+            r, t = batches[b][slot]
+            nc.vector.tensor_tensor(
+                picked_of[b][:, slot, :],
+                window_of[r][:].indirect(offsets[:, t * OFFSET_COLS : (t + 1) * OFFSET_COLS]),
+                bias_wide[:, r, :],
+                ADD,
+            )
+            if slot < len(batches[b]) - 1:
+                return
+            r, t = batches[b][0]
+            if r >= 2 * HEADS:
+                v_of[t] = per_patch.tile([PART, HEADS, PATCH], BF16, name="v_bf")
+                nc.gpsimd.tensor_copy(v_of[t][:], picked_of[b][:])
+                return
+            if t == 0 and r < HEADS:
+                rounded_of[r] = per_head.tile([PART, PATCHES, PATCH], BF16, name="q_bf")
+            if t == 0 and r >= HEADS:
+                rounded_of[r] = per_head.tile([PART, PATCHES, KEY_PITCH], BF16, name="k_bf")
                 nc.gpsimd.tensor_copy(
-                    rounded[:, u * PATCHES_PER_CLOUD : (u + 1) * PATCHES_PER_CLOUD, 0:PATCH], picked[:]
+                    rounded_of[r][:, :, PATCH:KEYS].rearrange("p (u t) o -> p u (t o)", u=CLOUDS),
+                    cq[:, r - HEADS, :].unsqueeze(2).to_broadcast([PART, CLOUDS, PATCHES_PER_CLOUD]),
                 )
+            nc.gpsimd.tensor_copy(rounded_of[r][:, t : t + PATCHES_PER_CLOUD, 0:PATCH], picked_of[b][:])
 
-        def project_class_tokens(r):
-            cq_ps = logits.tile([PART, KEYS], F32, name="cq_ps", tag="e_ps")
-            for cb in range(C_BLOCKS):
+        def logits(i):
+            h, t = units[i]
+            e_of[i] = []
+            for jb in range(HALVES):
+                e_ps = logit_banks.tile([PART, KEYS], F32, name="e_ps")
                 nc.tensor.matmul(
-                    cq_ps[:, 0:CLOUDS],
-                    lhsT=wqkv_sb[:, cb, r * PART : (r + 1) * PART],
-                    rhs=cls_sb[:, cb, :],
-                    start=(cb == 0),
-                    stop=(cb == C_BLOCKS - 1),
+                    e_ps[:],
+                    lhsT=rounded_of[h][:, t, jb * PART : (jb + 1) * PART],
+                    rhs=rounded_of[HEADS + h][:, t, 0:KEYS],
+                    start=True,
+                    stop=True,
                 )
-            return cq_ps
+                e_of[i].append(e_ps)
 
-        def softmax_weights(h, q_bf, k_bf, pair):
-            w = per_pair.tile([PART, PAIR, HALVES, KEY_PITCH], BF16, name="w")
-            for i in range(PAIR):
-                t = pair * PAIR + i
-                top = stats.tile([PART, HALVES], F32, name="top")
-                shift = stats.tile([PART, HALVES], F32, name="shift")
-                total = stats.tile([PART, HALVES], F32, name="total")
-                recip = stats.tile([PART, HALVES], F32, name="recip")
-                e_tiles = []
-                for jb in range(HALVES):
-                    e_ps = logits.tile([PART, KEYS], F32, name="e_ps")
-                    nc.tensor.matmul(
-                        e_ps[:],
-                        lhsT=q_bf[:, t, jb * PART : (jb + 1) * PART],
-                        rhs=k_bf[:, t, 0:KEYS],
-                        start=True,
-                        stop=True,
-                    )
-                    nc.vector.reduce_max(out=top[:, jb : jb + 1], in_=e_ps[:], axis=ALONG_FREE)
-                    e_tiles.append(e_ps)
-                nc.vector.tensor_scalar(out=shift[:], in0=top[:], scalar1=-SCALE, scalar2=None, op0=MULT)
-                ex_tiles = []
-                for jb in range(HALVES):
-                    ex = exps.tile([PART, KEYS], F32, name="ex")
-                    nc.scalar.activation(
-                        out=ex[:],
-                        in_=e_tiles[jb][:],
-                        func=EXP,
-                        bias=shift[:, jb : jb + 1],
-                        scale=SCALE,
-                        accum_out=total[:, jb : jb + 1],
-                    )
-                    ex_tiles.append(ex)
-                nc.vector.reciprocal(recip[:], total[:])
-                for jb in range(HALVES):
-                    nc.gpsimd.tensor_scalar(
-                        out=w[:, i, jb, 0:KEYS],
-                        in0=ex_tiles[jb][:],
-                        scalar1=recip[:, jb : jb + 1],
-                        scalar2=1.0,
-                        op0=MULT,
-                        op1=MULT,
-                    )
-            patches = slice(pair * PAIR, (pair + 1) * PAIR)
-            nc.gpsimd.tensor_copy(cls_w[:, patches, :, h], w[:, :, :, PATCH])
-            wT_ps = flips.tile([PART, PAIR, HALVES, PATCH], BF16, name="wT_ps", tag="flip_ps")
-            for i in range(PAIR):
+        def maxima(i):
+            top = stats.tile([PART, HALVES], F32, name="top")
+            for jb in range(HALVES):
+                nc.vector.reduce_max(out=top[:, jb : jb + 1], in_=e_of[i][jb][:], axis=ALONG_FREE)
+            shift_of[i] = stats.tile([PART, HALVES], F32, name="shift")
+            nc.vector.tensor_scalar(out=shift_of[i][:], in0=top[:], scalar1=-SCALE, scalar2=None, op0=MULT)
+
+        def exponentials(i):
+            total_of[i] = stats.tile([PART, HALVES], F32, name="total")
+            ex_of[i] = []
+            for jb in range(HALVES):
+                ex = exps.tile([PART, KEYS], F32, name="ex")
+                nc.scalar.activation(
+                    out=ex[:],
+                    in_=e_of[i][jb][:],
+                    func=EXP,
+                    bias=shift_of[i][:, jb : jb + 1],
+                    scale=SCALE,
+                    accum_out=total_of[i][:, jb : jb + 1],
+                )
+                ex_of[i].append(ex)
+
+        def reciprocals(i):
+            recip_of[i] = stats.tile([PART, HALVES], F32, name="recip")
+            nc.vector.reciprocal(recip_of[i][:], total_of[i][:])
+
+        def divide(i):
+            h, t = units[i]
+            pair, place = divmod(i, 2)
+            if place == 0:
+                w_of[pair] = per_pair.tile([PART, 2, HALVES, KEY_PITCH], BF16, name="w")
+            w = w_of[pair]
+            for jb in range(HALVES):
+                nc.gpsimd.tensor_scalar(
+                    out=w[:, place, jb, 0:KEYS],
+                    in0=ex_of[i][jb][:],
+                    scalar1=recip_of[i][:, jb : jb + 1],
+                    scalar2=1.0,
+                    op0=MULT,
+                    op1=MULT,
+                )
+            nc.gpsimd.tensor_copy(cls_w[:, t, :, h], w[:, place, :, PATCH])
+
+        def flip_weights(pair):
+            wT_ps = flips.tile([PART, 2, HALVES, PATCH], BF16, name="wT_ps", tag="flip_ps")
+            for place in range(2):
                 for ib in range(HALVES):
                     for jb in range(HALVES):
                         nc.tensor.transpose(
-                            wT_ps[:, i, ib, jb * PART : (jb + 1) * PART],
-                            w[:, i, jb, ib * PART : (ib + 1) * PART],
+                            wT_ps[:, place, ib, jb * PART : (jb + 1) * PART],
+                            w_of[pair][:, place, jb, ib * PART : (ib + 1) * PART],
                             ident[:],
                         )
-            nc.scalar.copy(wT[:, h, patches, :, :], wT_ps[:])
+            nc.scalar.copy(wT[:, 2 * pair : 2 * pair + 2, :, :], wT_ps[:])
 
-        def flip_class_weights(pair):
-            cls_wT_ps = flips.tile([PART, PAIR, PATCH], BF16, name="cls_wT_ps", tag="flip_ps")
-            for i in range(PAIR):
-                for jb in range(HALVES):
-                    nc.tensor.transpose(
-                        cls_wT_ps[:, i, jb * PART : (jb + 1) * PART], cls_w[:, pair * PAIR + i, jb, :], ident[:]
-                    )
-            cls_wT = per_pair.tile([PART, PAIR, PATCH], BF16, name="cls_wT")
-            nc.scalar.copy(cls_wT[:], cls_wT_ps[:])
-            return cls_wT
+        def flip_class_weights(t):
+            cls_wT_ps = flips.tile([PART, PATCH], BF16, name="cls_wT_ps", tag="flip_ps")
+            for jb in range(HALVES):
+                nc.tensor.transpose(cls_wT_ps[:, jb * PART : (jb + 1) * PART], cls_w[:, t, jb, :], ident[:])
+            cls_wT_of[t] = per_patch.tile([PART, PATCH], BF16, name="cls_wT")
+            nc.scalar.copy(cls_wT_of[t][:], cls_wT_ps[:])
 
-        def attend(t, cls_wT_t):
-            u = t // PATCHES_PER_CLOUD
-            picked_v = per_patch.tile([PART, HEADS, PATCH], F32, name="picked_v")
-            for h in range(HEADS):
-                look_up(picked_v[:, h, :], 2 * HEADS + h, value_windows[h], t)
-            v_bf = per_patch.tile([PART, HEADS, PATCH], BF16, name="v_bf")
-            nc.gpsimd.tensor_copy(v_bf[:], picked_v[:])
+        def flip_values(t):
             vT_ps = flips.tile([PART, HALVES, HEADS, DH], BF16, name="vT_ps", tag="flip_ps")
             for h in range(HEADS):
                 for ib in range(HALVES):
-                    nc.tensor.transpose(vT_ps[:, ib, h, :], v_bf[:, h, ib * PART : (ib + 1) * PART], ident[:])
-            vT = per_patch.tile([PART, HALVES, HEADS, DH], BF16, name="vT")
-            nc.scalar.copy(vT[:], vT_ps[:])
-            for first in range(0, HEADS, 2):
-                att_ps = logits.tile([PART, 2, PATCH], F32, name="att_ps", tag="e_ps")
-                for i in range(2):
-                    h = first + i
-                    for ib in range(HALVES):
-                        nc.tensor.matmul(
-                            att_ps[:, i, :], lhsT=vT[:, ib, h, :], rhs=wT[:, h, t, ib, :], start=(ib == 0), stop=False
-                        )
-                    nc.tensor.matmul(att_ps[:, i, :], lhsT=cv_rows[:, u, h, :], rhs=cls_wT_t, start=False, stop=True)
-                nc.scalar.copy(att_bf[:, first : first + 2, t * PATCH : (t + 1) * PATCH], att_ps[:])
+                    nc.tensor.transpose(vT_ps[:, ib, h, :], v_of[t][:, h, ib * PART : (ib + 1) * PART], ident[:])
+            vT_of[t] = per_patch.tile([PART, HALVES, HEADS, DH], BF16, name="vT")
+            nc.vector.tensor_copy(vT_of[t][:], vT_ps[:])
 
-        def project_out(n):
-            cols = slice(n * CHUNK, (n + 1) * CHUNK)
-            for m in range(C_BLOCKS):
-                out_ps = sums.tile([PART, CHUNK], F32, name="out_ps", tag="sum_ps")
+        def weighted_sums(t, first):
+            u = t // PATCHES_PER_CLOUD
+            att_ps = sums.tile([PART, 2, PATCH], F32, name="att_ps", tag="sum_ps")
+            for i in range(2):
+                h = first + i
+                for ib in range(HALVES):
+                    nc.tensor.matmul(
+                        att_ps[:, i, :],
+                        lhsT=vT_of[t][:, ib, h, :],
+                        rhs=wT[:, unit_of[(h, t)], ib, :],
+                        start=(ib == 0),
+                        stop=False,
+                    )
+                nc.tensor.matmul(att_ps[:, i, :], lhsT=cv_rows[:, u, h, :], rhs=cls_wT_of[t][:], start=False, stop=True)
+            nc.scalar.copy(att_bf[:, first : first + 2, t * PATCH : (t + 1) * PATCH], att_ps[:])
+
+        def project_out(t, first):
+            cols = slice(t * PATCH, (t + 1) * PATCH)
+            out_ps = sums.tile([PART, 2, PATCH], F32, name="out_ps", tag="sum_ps")
+            out_sb = results.tile([PART, 2, PATCH], F32, name="out_sb")
+            for i in range(2):
+                m = first + i
                 for h in range(HEADS):
                     nc.tensor.matmul(
-                        out_ps[:],
+                        out_ps[:, i, :],
                         lhsT=wproj_sb[:, h, m * PART : (m + 1) * PART],
                         rhs=att_bf[:, h, cols],
                         start=(h == 0),
                         stop=(h == HEADS - 1),
                     )
-                out_sb = results.tile([PART, CHUNK], F32, name="out_sb")
                 nc.scalar.activation(
-                    out=out_sb[:], in_=out_ps[:], func=IDENTITY, bias=bias[:, ROW_BLOCKS + m : ROW_BLOCKS + m + 1]
+                    out=out_sb[:, i, :],
+                    in_=out_ps[:, i, :],
+                    func=IDENTITY,
+                    bias=bias[:, ROW_BLOCKS + m : ROW_BLOCKS + m + 1],
                 )
-                nc.sync.dma_start(out[m * PART : (m + 1) * PART, cols], out_sb[:])
+            nc.sync.dma_start(out.rearrange("(m p) j -> p m j", p=PART)[:, first : first + 2, cols], out_sb[:])
 
-        q_of = {}
-        k_of = {}
+        first_projections = 3 * CHUNKS
+        first_pieces = 2 * PATCHES_PER_CLOUD
+        for n in range(CHUNKS):
+            for s in (2 * n, 2 * n + 1):
+                round_slice(s)
+                if s + STAGED < POINTS // SLICE:
+                    load_slice(s + STAGED)
+            for r, m in projections[2 * n : 2 * n + 2]:
+                project_chunk(r, m)
+        nc.sync.dma_start(wqkv_sb[:, :, 2 * C : 3 * C], wqkv_blocks[:, :, 2 * C : 3 * C])
+        nc.sync.dma_start(wproj_sb[:], wproj.rearrange("(cb p) m -> p cb m", p=PART))
+        cq_ps = logit_banks.tile([PART, KEYS], F32, name="cq_ps", tag="e_ps")
+        cq_sums = cq_ps[:, 0 : 2 * HEADS * CLOUDS].rearrange("p (b u) -> p b u", u=CLOUDS)
+        for g in range(2 * HEADS):
+            for cb in range(C_BLOCKS):
+                nc.tensor.matmul(
+                    cq_sums[:, g, :],
+                    lhsT=wqkv_sb[:, cb, (HEADS + g) * PART : (HEADS + g + 1) * PART],
+                    rhs=cls_sb[:, cb, :],
+                    start=(cb == 0),
+                    stop=(cb == C_BLOCKS - 1),
+                )
+        for b, slot in pieces[0:PATCHES_PER_CLOUD]:
+            look_up(b, slot)
+        nc.vector.tensor_tensor(
+            cq[:], cq_sums, bias[:, HEADS:ROW_BLOCKS].unsqueeze(2).to_broadcast([PART, 2 * HEADS, CLOUDS]), ADD
+        )
         for h in range(HEADS):
-            q_of[h] = per_head.tile([PART, PATCHES, PATCH], BF16, name="q_bf")
-            k_of[h] = per_head.tile([PART, PATCHES, KEY_PITCH], BF16, name="k_bf")
-            q_window = windows.tile([PART, POINTS], F32, name="q_window", tag="window")
-            k_window = windows.tile([PART, POINTS], F32, name="k_window", tag="window")
-            blocks = ((h, q_window, q_of[h]), (HEADS + h, k_window, k_of[h]), (2 * HEADS + h, value_windows[h], None))
-            if h == 0:
-                jobs = [(b, n) for n in range(CHUNKS) for b in (0, 1)] + [(2, n) for n in range(CHUNKS)]
-            else:
-                jobs = [(b, n) for b in range(3) for n in range(CHUNKS)]
-            share = len(jobs) // CHUNKS
-            for pair in range(CHUNKS):
-                if h > 0:
-                    softmax_weights(h - 1, q_of[h - 1], k_of[h - 1], pair)
-                for b, n in jobs[pair * share : (pair + 1) * share]:
-                    r, window, rounded = blocks[b]
-                    project_chunk(r, n, window)
-                    if n == CHUNKS - 1 and rounded is not None:
-                        look_up_rows(r, window, rounded)
+            nc.gpsimd.tensor_copy(cv_cols[:, :, h, h], cq[:, HEADS + h, :])
+        for b, slot in pieces[PATCHES_PER_CLOUD:first_pieces]:
+            look_up(b, slot)
+        for r, n in projections[2 * CHUNKS : first_projections]:
+            project_chunk(r, n)
+        cv_ps = flips.tile([PART, CLOUDS, HEADS, DH], BF16, name="cv_ps", tag="flip_ps")
+        for u in range(CLOUDS):
+            for h in range(HEADS):
+                nc.tensor.transpose(cv_ps[:, u, h, :], cv_cols[:, u, h, :], ident[:])
+        nc.scalar.copy(cv_rows[:], cv_ps[:])
 
-            if h == 0:
-                ck = held.tile([PART, HEADS, CLOUDS], F32, name="ck")
-                for g in range(HEADS):
-                    r = HEADS + g
-                    cq_ps = project_class_tokens(r)
-                    nc.vector.tensor_scalar(
-                        out=ck[:, g, :], in0=cq_ps[:, 0:CLOUDS], scalar1=bias[:, r : r + 1], scalar2=None, op0=ADD
-                    )
-                cv_cols = held.tile([PART, CLOUDS, HEADS, PART], BF16, name="cv_cols")
-                nc.gpsimd.memset(cv_cols[:], 0.0)
-                for g in range(HEADS):
-                    r = 2 * HEADS + g
-                    cq_ps = project_class_tokens(r)
-                    nc.vector.tensor_scalar(
-                        out=cv_cols[:, :, g, g], in0=cq_ps[:, 0:CLOUDS], scalar1=bias[:, r : r + 1], scalar2=None, op0=ADD
-                    )
-                cv_ps = flips.tile([PART, CLOUDS, HEADS, DH], BF16, name="cv_ps", tag="flip_ps")
-                for u in range(CLOUDS):
-                    for g in range(HEADS):
-                        nc.tensor.transpose(cv_ps[:, u, g, :], cv_cols[:, u, g, :], ident[:])
-                cv_rows = held.tile([PART, CLOUDS, HEADS, DH], BF16, name="cv_rows")
-                nc.vector.tensor_copy(cv_rows[:], cv_ps[:])
-
-            nc.gpsimd.tensor_copy(
-                k_of[h][:, :, PATCH:KEYS].rearrange("p (u t) o -> p u (t o)", u=CLOUDS),
-                ck[:, h, :].unsqueeze(2).to_broadcast([PART, CLOUDS, PATCHES_PER_CLOUD]),
-            )
-
-        last = HEADS - 1
-        for pair in range(CHUNKS):
-            softmax_weights(last, q_of[last], k_of[last], pair)
-            cls_wT = flip_class_weights(pair)
-            for i in range(PAIR):
-                attend(pair * PAIR + i, cls_wT[:, i, :])
-            project_out(pair)
+        last_lag = 9
+        for tick in range(len(units) + last_lag + 1):
+            if tick < len(units):
+                logits(tick)
+            if 0 <= tick - 1 < len(units):
+                exponentials(tick - 1)
+            if 0 <= tick - 2 < len(units):
+                divide(tick - 2)
+            for r, n in projections[first_projections + 2 * tick : first_projections + 2 * tick + 2]:
+                project_chunk(r, n)
+            for b, slot in pieces[first_pieces + 3 * tick : first_pieces + 3 * tick + 3]:
+                look_up(b, slot)
+            if tick < len(units):
+                maxima(tick)
+            if 0 <= tick - 1 < len(units):
+                reciprocals(tick - 1)
+            if 0 <= tick - 3 < len(units) and (tick - 3) % 2 == 1:
+                flip_weights((tick - 3) // 2)
+            if tick - 3 in patch_ending_at:
+                flip_class_weights(patch_ending_at[tick - 3])
+            if tick - 4 in patch_ending_at:
+                flip_values(patch_ending_at[tick - 4])
+            if tick - 6 in patch_ending_at:
+                weighted_sums(patch_ending_at[tick - 6], 0)
+            if tick - 7 in patch_ending_at:
+                weighted_sums(patch_ending_at[tick - 7], 2)
+            if tick - 8 in patch_ending_at:
+                project_out(patch_ending_at[tick - 8], 0)
+            if tick - last_lag in patch_ending_at:
+                project_out(patch_ending_at[tick - last_lag], 2)

@@ -111,6 +111,7 @@ def tile_serializedattention_b_kernel(tc, feat, cls_tok, wqkv, bqkv, wproj, bpro
         ]
         unit_of = {unit: i for i, unit in enumerate(units)}
         patch_ending_at = {unit_of[(HEADS - 1, t)]: t for t in range(PATCHES)}
+        chunk_ending_at = {unit_of[(HEADS - 1, 2 * n + 1)]: n for n in range(CHUNKS)}
 
         row_order = [r for h in range(HEADS) for r in (h, HEADS + h)] + [2 * HEADS + h for h in range(HEADS)]
         projections = [(r, n) for n in range(CHUNKS) for r in row_order[0:2]] + [
@@ -282,27 +283,22 @@ def tile_serializedattention_b_kernel(tc, feat, cls_tok, wqkv, bqkv, wproj, bpro
                 nc.tensor.matmul(att_ps[:, i, :], lhsT=cv_rows[:, u, h, :], rhs=cls_wT_of[t][:], start=False, stop=True)
             nc.scalar.copy(att_bf[:, first : first + 2, t * PATCH : (t + 1) * PATCH], att_ps[:])
 
-        def project_out(t, first):
-            cols = slice(t * PATCH, (t + 1) * PATCH)
-            out_ps = sums.tile([PART, 2, PATCH], F32, name="out_ps", tag="sum_ps")
-            out_sb = results.tile([PART, 2, PATCH], F32, name="out_sb")
-            for i in range(2):
-                m = first + i
-                for h in range(HEADS):
-                    nc.tensor.matmul(
-                        out_ps[:, i, :],
-                        lhsT=wproj_sb[:, h, m * PART : (m + 1) * PART],
-                        rhs=att_bf[:, h, cols],
-                        start=(h == 0),
-                        stop=(h == HEADS - 1),
-                    )
-                nc.scalar.activation(
-                    out=out_sb[:, i, :],
-                    in_=out_ps[:, i, :],
-                    func=IDENTITY,
-                    bias=bias[:, ROW_BLOCKS + m : ROW_BLOCKS + m + 1],
+        def project_out(n, m):
+            cols = slice(n * CHUNK, (n + 1) * CHUNK)
+            out_ps = sums.tile([PART, CHUNK], F32, name="out_ps", tag="sum_ps")
+            for h in range(HEADS):
+                nc.tensor.matmul(
+                    out_ps[:],
+                    lhsT=wproj_sb[:, h, m * PART : (m + 1) * PART],
+                    rhs=att_bf[:, h, cols],
+                    start=(h == 0),
+                    stop=(h == HEADS - 1),
                 )
-            nc.sync.dma_start(out.rearrange("(m p) j -> p m j", p=PART)[:, first : first + 2, cols], out_sb[:])
+            out_sb = results.tile([PART, CHUNK], F32, name="out_sb")
+            nc.scalar.activation(
+                out=out_sb[:], in_=out_ps[:], func=IDENTITY, bias=bias[:, ROW_BLOCKS + m : ROW_BLOCKS + m + 1]
+            )
+            nc.sync.dma_start(out[m * PART : (m + 1) * PART, cols], out_sb[:])
 
         first_projections = 3 * CHUNKS
         first_pieces = 2 * PATCHES_PER_CLOUD
@@ -343,7 +339,7 @@ def tile_serializedattention_b_kernel(tc, feat, cls_tok, wqkv, bqkv, wproj, bpro
                 nc.tensor.transpose(cv_ps[:, u, h, :], cv_cols[:, u, h, :], ident[:])
         nc.scalar.copy(cv_rows[:], cv_ps[:])
 
-        last_lag = 9
+        last_lag = 8 + C_BLOCKS - 1
         for tick in range(len(units) + last_lag + 1):
             if tick < len(units):
                 logits(tick)
@@ -361,15 +357,13 @@ def tile_serializedattention_b_kernel(tc, feat, cls_tok, wqkv, bqkv, wproj, bpro
                 reciprocals(tick - 1)
             if 0 <= tick - 3 < len(units) and (tick - 3) % 2 == 1:
                 flip_weights((tick - 3) // 2)
-            if tick - 3 in patch_ending_at:
-                flip_class_weights(patch_ending_at[tick - 3])
             if tick - 4 in patch_ending_at:
+                flip_class_weights(patch_ending_at[tick - 4])
                 flip_values(patch_ending_at[tick - 4])
             if tick - 6 in patch_ending_at:
                 weighted_sums(patch_ending_at[tick - 6], 0)
             if tick - 7 in patch_ending_at:
                 weighted_sums(patch_ending_at[tick - 7], 2)
-            if tick - 8 in patch_ending_at:
-                project_out(patch_ending_at[tick - 8], 0)
-            if tick - last_lag in patch_ending_at:
-                project_out(patch_ending_at[tick - last_lag], 2)
+            for m in range(C_BLOCKS):
+                if tick - 8 - m in chunk_ending_at:
+                    project_out(chunk_ending_at[tick - 8 - m], m)

@@ -171,17 +171,17 @@ def tile_serializedattention_b_kernel(tc, feat, cls_tok, wqkv, bqkv, wproj, bpro
             r, t = batches[b][0]
             if r >= 2 * HEADS:
                 v_of[t] = per_patch.tile([PART, HEADS, PATCH], BF16, name="v_bf")
-                nc.gpsimd.tensor_copy(v_of[t][:], picked_of[b][:])
+                nc.vector.tensor_copy(v_of[t][:], picked_of[b][:])
                 return
             if t == 0 and r < HEADS:
                 rounded_of[r] = per_head.tile([PART, PATCHES, PATCH], BF16, name="q_bf")
             if t == 0 and r >= HEADS:
                 rounded_of[r] = per_head.tile([PART, PATCHES, KEY_PITCH], BF16, name="k_bf")
-                nc.gpsimd.tensor_copy(
+                nc.vector.tensor_copy(
                     rounded_of[r][:, :, PATCH:KEYS].rearrange("p (u t) o -> p u (t o)", u=CLOUDS),
                     cq[:, r - HEADS, :].unsqueeze(2).to_broadcast([PART, CLOUDS, PATCHES_PER_CLOUD]),
                 )
-            nc.gpsimd.tensor_copy(rounded_of[r][:, t : t + PATCHES_PER_CLOUD, 0:PATCH], picked_of[b][:])
+            nc.vector.tensor_copy(rounded_of[r][:, t : t + PATCHES_PER_CLOUD, 0:PATCH], picked_of[b][:])
 
         def logits(i):
             h, t = units[i]

@@ -10,6 +10,7 @@ ADD = mybir.AluOpType.add
 MULT = mybir.AluOpType.mult
 EXP = mybir.ActivationFunctionType.Exp
 IDENTITY = mybir.ActivationFunctionType.Identity
+COPY = mybir.ActivationFunctionType.Copy
 ALONG_FREE = mybir.AxisListType.X
 
 PART = 128
@@ -230,15 +231,10 @@ def tile_serializedattention_b_kernel(tc, feat, cls_tok, wqkv, bqkv, wproj, bpro
                 w_of[pair] = per_pair.tile([PART, 2, HALVES, KEY_PITCH], BF16, name="w")
             w = w_of[pair]
             for jb in range(HALVES):
-                nc.gpsimd.tensor_scalar(
-                    out=w[:, place, jb, 0:KEYS],
-                    in0=ex_of[i][jb][:],
-                    scalar1=recip_of[i][:, jb : jb + 1],
-                    scalar2=1.0,
-                    op0=MULT,
-                    op1=MULT,
+                nc.scalar.activation(
+                    out=w[:, place, jb, 0:KEYS], in_=ex_of[i][jb][:], func=COPY, scale=recip_of[i][:, jb : jb + 1]
                 )
-            nc.gpsimd.tensor_copy(cls_w[:, t, :, h], w[:, place, :, PATCH])
+            nc.vector.tensor_copy(cls_w[:, t, :, h], w[:, place, :, PATCH])
 
         def flip_weights(pair):
             wT_ps = flips.tile([PART, 2, HALVES, PATCH], BF16, name="wT_ps", tag="flip_ps")

@@ -20,6 +20,7 @@ HEADS = 4
 DH = C // HEADS
 PATCH = 256
 PATCHES = POINTS // PATCH
+UNITS = HEADS * PATCHES
 CLOUDS = 2
 PATCHES_PER_CLOUD = PATCHES // CLOUDS
 KEYS = PATCH + 1
@@ -31,9 +32,11 @@ CHUNKS = POINTS // CHUNK
 SLICE = CHUNK // 2
 STAGED = 4
 HALVES = PATCH // PART
-OFFSET_COLS = PATCH // 16
+PAIR = 2
+PIECE = PAIR * PATCH
+PIECES = POINTS // PIECE
+OFFSET_COLS = PIECE // 16
 SCALE = DH**-0.5
-EARLY_HEADS = 2
 
 FLOPS = (
     2 * C * 3 * C * POINTS
@@ -49,16 +52,17 @@ def tile_serializedattention_b_kernel(tc, feat, cls_tok, wqkv, bqkv, wproj, bpro
         held = ctx.enter_context(tc.tile_pool(name="held", bufs=1))
         stage = ctx.enter_context(tc.tile_pool(name="stage", bufs=STAGED))
         windows = ctx.enter_context(tc.tile_pool(name="windows", bufs=6))
-        picks = ctx.enter_context(tc.tile_pool(name="picks", bufs=3))
-        per_head = ctx.enter_context(tc.tile_pool(name="per_head", bufs=3))
-        stats = ctx.enter_context(tc.tile_pool(name="stats", bufs=4))
+        picks = ctx.enter_context(tc.tile_pool(name="picks", bufs=2))
+        per_head = ctx.enter_context(tc.tile_pool(name="per_head", bufs=2))
+        stats = ctx.enter_context(tc.tile_pool(name="stats", bufs=8))
         exps = ctx.enter_context(tc.tile_pool(name="exps", bufs=6))
-        per_pair = ctx.enter_context(tc.tile_pool(name="per_pair", bufs=3))
-        per_patch = ctx.enter_context(tc.tile_pool(name="per_patch", bufs=3))
-        results = ctx.enter_context(tc.tile_pool(name="results", bufs=3))
+        per_unit = ctx.enter_context(tc.tile_pool(name="per_unit", bufs=3))
+        diagonals = ctx.enter_context(tc.tile_pool(name="diagonals", bufs=6))
+        results = ctx.enter_context(tc.tile_pool(name="results", bufs=4))
         sums = ctx.enter_context(tc.psum_pool(name="sums", bufs=2))
         logit_banks = ctx.enter_context(tc.psum_pool(name="logit_banks", bufs=4))
-        flips = ctx.enter_context(tc.psum_pool(name="flips", bufs=2))
+        flips = ctx.enter_context(tc.psum_pool(name="flips", bufs=1))
+        att_banks = ctx.enter_context(tc.psum_pool(name="att_banks", bufs=1))
 
         offsets = held.tile([PART, POINTS // 16], U16, name="offsets")
         wqkv_sb = held.tile([PART, C_BLOCKS, 3 * C], BF16, name="wqkv_sb")
@@ -86,6 +90,7 @@ def tile_serializedattention_b_kernel(tc, feat, cls_tok, wqkv, bqkv, wproj, bpro
         nc.sync.dma_start(wqkv_sb[:, :, 0 : 2 * C], wqkv_blocks[:, :, 0 : 2 * C])
         for s in range(STAGED):
             load_slice(s)
+        nc.scalar.dma_start(wqkv_sb[:, :, 2 * C : 3 * C], wqkv_blocks[:, :, 2 * C : 3 * C])
         nc.sync.dma_start(offsets[:], offs)
 
         zero = held.tile([PART, 1], F32, name="zero")
@@ -102,45 +107,28 @@ def tile_serializedattention_b_kernel(tc, feat, cls_tok, wqkv, bqkv, wproj, bpro
         nc.tensor.transpose(bias_ps[:, 0:PART], bias_rows[:], ident_f32[:])
         bias = held.tile([PART, ROW_BLOCKS + C_BLOCKS], F32, name="bias")
         nc.vector.tensor_copy(bias[:], bias_ps[:, 0 : ROW_BLOCKS + C_BLOCKS])
-        bias_wide = held.tile([PART, ROW_BLOCKS, PATCH], F32, name="bias_wide")
-        nc.gpsimd.tensor_copy(
-            bias_wide[:], bias[:, 0:ROW_BLOCKS].unsqueeze(2).to_broadcast([PART, ROW_BLOCKS, PATCH])
-        )
+        bias_wide = held.tile([PART, ROW_BLOCKS, PIECE], F32, name="bias_wide")
 
-        units = [(h, t) for h in range(EARLY_HEADS) for t in range(PATCHES)] + [
-            (h, t) for t in range(PATCHES) for h in range(EARLY_HEADS, HEADS)
-        ]
-        unit_of = {unit: i for i, unit in enumerate(units)}
-        patch_ending_at = {unit_of[(HEADS - 1, t)]: t for t in range(PATCHES)}
-        chunk_ending_at = {unit_of[(HEADS - 1, 2 * n + 1)]: n for n in range(CHUNKS)}
+        def spread_bias(engine, r):
+            engine.tensor_copy(bias_wide[:, r, :], bias[:, r : r + 1].to_broadcast([PART, PIECE]))
 
-        row_order = [r for h in range(HEADS) for r in (h, HEADS + h)] + [2 * HEADS + h for h in range(HEADS)]
+        row_order = [r for h in range(HEADS) for r in (h, HEADS + h, 2 * HEADS + h)]
         projections = [(r, n) for n in range(CHUNKS) for r in row_order[0:2]] + [
             (r, n) for r in row_order[2:] for n in range(CHUNKS)
         ]
-        batches = [
-            [(r, u * PATCHES_PER_CLOUD + i) for i in range(PATCHES_PER_CLOUD)]
-            for h in range(HEADS)
-            for u in range(CLOUDS)
-            for r in (h, HEADS + h)
-        ] + [[(2 * HEADS + h, t) for h in range(HEADS)] for t in range(PATCHES)]
-        pieces = [(b, slot) for b in range(len(batches)) for slot in range(len(batches[b]))]
 
-        wT = held.tile([PART, len(units), HALVES, PATCH], BF16, name="wT")
-        cls_w = held.tile([PART, PATCHES, HALVES, PART], BF16, name="cls_w")
-        nc.gpsimd.memset(cls_w[:], 0.0)
-        cv_cols = held.tile([PART, CLOUDS, HEADS, PART], BF16, name="cv_cols")
-        nc.gpsimd.memset(cv_cols[:], 0.0)
-        cv_rows = held.tile([PART, CLOUDS, HEADS, DH], BF16, name="cv_rows")
         cq = held.tile([PART, 2 * HEADS, CLOUDS], F32, name="cq")
+        cv_spread = held.tile([PART, HEADS, CLOUDS, PART], BF16, name="cv_spread")
+        cv_rows = held.tile([PART, HEADS, CLOUDS, DH], BF16, name="cv_rows")
         att_bf = held.tile([PART, HEADS, POINTS], BF16, name="att_bf")
 
         window_of = {}
-        rounded_of = {}
-        picked_of = {}
-        v_of, vT_of, cls_wT_of = {}, {}, {}
+        picked_qk_of = {}
+        qk_of, v_of = {}, {}
         e_of, shift_of, ex_of, total_of, recip_of = {}, {}, {}, {}, {}
-        w_of = {}
+        w_of, diag_of = {}, {}
+        flip_ps_of, flipped_of = {}, {}
+        att_ps_of = {}
 
         def project_chunk(r, n):
             if n == 0:
@@ -157,42 +145,47 @@ def tile_serializedattention_b_kernel(tc, feat, cls_tok, wqkv, bqkv, wproj, bpro
                 )
             nc.scalar.copy(window_of[r][:, cols], p_ps[:])
 
-        def look_up(b, slot):
-            if slot == 0:
-                picked_of[b] = picks.tile([PART, len(batches[b]), PATCH], F32, name="picked")
-            r, t = batches[b][slot]
+        def look_up(dest, r, g):
             nc.vector.tensor_tensor(
-                picked_of[b][:, slot, :],
-                window_of[r][:].indirect(offsets[:, t * OFFSET_COLS : (t + 1) * OFFSET_COLS]),
+                dest,
+                window_of[r][:].indirect(offsets[:, g * OFFSET_COLS : (g + 1) * OFFSET_COLS]),
                 bias_wide[:, r, :],
                 ADD,
             )
-            if slot < len(batches[b]) - 1:
-                return
-            r, t = batches[b][0]
-            if r >= 2 * HEADS:
-                v_of[t] = per_patch.tile([PART, HEADS, PATCH], BF16, name="v_bf")
-                nc.vector.tensor_copy(v_of[t][:], picked_of[b][:])
-                return
-            if t == 0 and r < HEADS:
-                rounded_of[r] = per_head.tile([PART, PATCHES, PATCH], BF16, name="q_bf")
-            if t == 0 and r >= HEADS:
-                rounded_of[r] = per_head.tile([PART, PATCHES, KEY_PITCH], BF16, name="k_bf")
+
+        def look_up_queries_and_keys(h, g):
+            if g == 0:
+                qk_of[h] = per_head.tile([PART, 2, PATCHES, KEY_PITCH], BF16, name="qk_bf")
                 nc.vector.tensor_copy(
-                    rounded_of[r][:, :, PATCH:KEYS].rearrange("p (u t) o -> p u (t o)", u=CLOUDS),
-                    cq[:, r - HEADS, :].unsqueeze(2).to_broadcast([PART, CLOUDS, PATCHES_PER_CLOUD]),
+                    qk_of[h][:, 1, :, PATCH:KEYS].rearrange("p (u t) o -> p u (t o)", u=CLOUDS),
+                    cq[:, h, :].unsqueeze(2).to_broadcast([PART, CLOUDS, PATCHES_PER_CLOUD]),
                 )
-            nc.vector.tensor_copy(rounded_of[r][:, t : t + PATCHES_PER_CLOUD, 0:PATCH], picked_of[b][:])
+            picked_qk_of[(h, g)] = picks.tile([PART, 2, PIECE], F32, name="picked_qk")
+            look_up(picked_qk_of[(h, g)][:, 0, :], h, g)
+            look_up(picked_qk_of[(h, g)][:, 1, :], HEADS + h, g)
+
+        def round_queries_and_keys(h, g):
+            nc.vector.tensor_copy(
+                qk_of[h][:, :, g * PAIR : (g + 1) * PAIR, 0:PATCH],
+                picked_qk_of[(h, g)][:].rearrange("p a (t j) -> p a t j", t=PAIR),
+            )
+
+        def look_up_values(h, g):
+            if g == 0:
+                v_of[h] = per_head.tile([PART, POINTS], BF16, name="v_bf")
+            picked_v = picks.tile([PART, PIECE], F32, name="picked_v")
+            look_up(picked_v[:], 2 * HEADS + h, g)
+            nc.vector.tensor_copy(v_of[h][:, g * PIECE : (g + 1) * PIECE], picked_v[:])
 
         def logits(i):
-            h, t = units[i]
+            h, t = divmod(i, PATCHES)
             e_of[i] = []
             for jb in range(HALVES):
                 e_ps = logit_banks.tile([PART, KEYS], F32, name="e_ps")
                 nc.tensor.matmul(
                     e_ps[:],
-                    lhsT=rounded_of[h][:, t, jb * PART : (jb + 1) * PART],
-                    rhs=rounded_of[HEADS + h][:, t, 0:KEYS],
+                    lhsT=qk_of[h][:, 0, t, jb * PART : (jb + 1) * PART],
+                    rhs=qk_of[h][:, 1, t, 0:KEYS],
                     start=True,
                     stop=True,
                 )
@@ -223,61 +216,70 @@ def tile_serializedattention_b_kernel(tc, feat, cls_tok, wqkv, bqkv, wproj, bpro
         def reciprocals(i):
             recip_of[i] = stats.tile([PART, HALVES], F32, name="recip")
             nc.vector.reciprocal(recip_of[i][:], total_of[i][:])
+            diag_of[i] = diagonals.tile([PART, HALVES, PART], BF16, name="diag")
+            for jb in range(HALVES):
+                nc.vector.tensor_scalar(
+                    out=diag_of[i][:, jb, :],
+                    in0=ident[:],
+                    scalar1=ex_of[i][jb][:, PATCH:KEYS],
+                    scalar2=recip_of[i][:, jb : jb + 1],
+                    op0=MULT,
+                    op1=MULT,
+                )
 
         def divide(i):
-            h, t = units[i]
-            pair, place = divmod(i, 2)
-            if place == 0:
-                w_of[pair] = per_pair.tile([PART, 2, HALVES, KEY_PITCH], BF16, name="w")
-            w = w_of[pair]
+            w_of[i] = per_unit.tile([PART, HALVES, PATCH], BF16, name="w")
             for jb in range(HALVES):
                 nc.scalar.activation(
-                    out=w[:, place, jb, 0:KEYS], in_=ex_of[i][jb][:], func=COPY, scale=recip_of[i][:, jb : jb + 1]
+                    out=w_of[i][:, jb, :], in_=ex_of[i][jb][:, 0:PATCH], func=COPY, scale=recip_of[i][:, jb : jb + 1]
                 )
-            nc.vector.tensor_copy(cls_w[:, t, :, h], w[:, place, :, PATCH])
 
-        def flip_weights(pair):
-            wT_ps = flips.tile([PART, 2, HALVES, PATCH], BF16, name="wT_ps", tag="flip_ps")
-            for place in range(2):
-                for ib in range(HALVES):
-                    for jb in range(HALVES):
-                        nc.tensor.transpose(
-                            wT_ps[:, place, ib, jb * PART : (jb + 1) * PART],
-                            w_of[pair][:, place, jb, ib * PART : (ib + 1) * PART],
-                            ident[:],
-                        )
-            nc.scalar.copy(wT[:, 2 * pair : 2 * pair + 2, :, :], wT_ps[:])
+        def flip(i):
+            h, t = divmod(i, PATCHES)
+            flip_ps = flips.tile([PART, HALVES * (PATCH + DH)], BF16, name="flip_ps")
+            for ib in range(HALVES):
+                for jb in range(HALVES):
+                    nc.tensor.transpose(
+                        flip_ps[:, ib * PATCH + jb * PART : ib * PATCH + (jb + 1) * PART],
+                        w_of[i][:, jb, ib * PART : (ib + 1) * PART],
+                        ident[:],
+                    )
+            for ib in range(HALVES):
+                nc.tensor.transpose(
+                    flip_ps[:, HALVES * PATCH + ib * DH : HALVES * PATCH + (ib + 1) * DH],
+                    v_of[h][:, t * PATCH + ib * PART : t * PATCH + (ib + 1) * PART],
+                    ident[:],
+                )
+            flip_ps_of[i] = flip_ps
 
-        def flip_class_weights(t):
-            cls_wT_ps = flips.tile([PART, PATCH], BF16, name="cls_wT_ps", tag="flip_ps")
-            for jb in range(HALVES):
-                nc.tensor.transpose(cls_wT_ps[:, jb * PART : (jb + 1) * PART], cls_w[:, t, jb, :], ident[:])
-            cls_wT_of[t] = per_patch.tile([PART, PATCH], BF16, name="cls_wT")
-            nc.scalar.copy(cls_wT_of[t][:], cls_wT_ps[:])
+        def copy_flipped(i):
+            flipped_of[i] = per_unit.tile([PART, HALVES * (PATCH + DH)], BF16, name="flipped")
+            nc.scalar.copy(flipped_of[i][:], flip_ps_of[i][:])
 
-        def flip_values(t):
-            vT_ps = flips.tile([PART, HALVES, HEADS, DH], BF16, name="vT_ps", tag="flip_ps")
-            for h in range(HEADS):
-                for ib in range(HALVES):
-                    nc.tensor.transpose(vT_ps[:, ib, h, :], v_of[t][:, h, ib * PART : (ib + 1) * PART], ident[:])
-            vT_of[t] = per_patch.tile([PART, HALVES, HEADS, DH], BF16, name="vT")
-            nc.vector.tensor_copy(vT_of[t][:], vT_ps[:])
-
-        def weighted_sums(t, first):
+        def weighted_sums(i):
+            h, t = divmod(i, PATCHES)
             u = t // PATCHES_PER_CLOUD
-            att_ps = sums.tile([PART, 2, PATCH], F32, name="att_ps", tag="sum_ps")
-            for i in range(2):
-                h = first + i
+            pair, place = divmod(i, PAIR)
+            if place == 0:
+                att_ps_of[pair] = att_banks.tile([PART, PIECE], F32, name="att_ps")
+            att_ps = att_ps_of[pair]
+            for jb in range(HALVES):
+                queries = slice(place * PATCH + jb * PART, place * PATCH + (jb + 1) * PART)
                 for ib in range(HALVES):
                     nc.tensor.matmul(
-                        att_ps[:, i, :],
-                        lhsT=vT_of[t][:, ib, h, :],
-                        rhs=wT[:, unit_of[(h, t)], ib, :],
+                        att_ps[:, queries],
+                        lhsT=flipped_of[i][:, HALVES * PATCH + ib * DH : HALVES * PATCH + (ib + 1) * DH],
+                        rhs=flipped_of[i][:, ib * PATCH + jb * PART : ib * PATCH + (jb + 1) * PART],
                         start=(ib == 0),
                         stop=False,
                     )
-                nc.tensor.matmul(att_ps[:, i, :], lhsT=cv_rows[:, u, h, :], rhs=cls_wT_of[t][:], start=False, stop=True)
-            nc.scalar.copy(att_bf[:, first : first + 2, t * PATCH : (t + 1) * PATCH], att_ps[:])
+                nc.tensor.matmul(
+                    att_ps[:, queries], lhsT=cv_rows[:, h, u, :], rhs=diag_of[i][:, jb, :], start=False, stop=True
+                )
+
+        def copy_weighted_sums(pair):
+            h, g = divmod(pair, PIECES)
+            nc.scalar.copy(att_bf[:, h, g * PIECE : (g + 1) * PIECE], att_ps_of[pair][:])
 
         def project_out(n, m):
             cols = slice(n * CHUNK, (n + 1) * CHUNK)
@@ -291,21 +293,25 @@ def tile_serializedattention_b_kernel(tc, feat, cls_tok, wqkv, bqkv, wproj, bpro
                     stop=(h == HEADS - 1),
                 )
             out_sb = results.tile([PART, CHUNK], F32, name="out_sb")
-            nc.scalar.activation(
-                out=out_sb[:], in_=out_ps[:], func=IDENTITY, bias=bias[:, ROW_BLOCKS + m : ROW_BLOCKS + m + 1]
-            )
+            bproj_m = bias[:, ROW_BLOCKS + m : ROW_BLOCKS + m + 1]
+            if m % 2 == 0:
+                nc.scalar.activation(out=out_sb[:], in_=out_ps[:], func=IDENTITY, bias=bproj_m)
+            else:
+                nc.vector.tensor_scalar(out=out_sb[:], in0=out_ps[:], scalar1=bproj_m, scalar2=None, op0=ADD)
             nc.sync.dma_start(out[m * PART : (m + 1) * PART, cols], out_sb[:])
 
         first_projections = 3 * CHUNKS
-        first_pieces = 2 * PATCHES_PER_CLOUD
+        for r in row_order[3:]:
+            spread_bias(nc.gpsimd, r)
         for n in range(CHUNKS):
             for s in (2 * n, 2 * n + 1):
                 round_slice(s)
                 if s + STAGED < POINTS // SLICE:
                     load_slice(s + STAGED)
+            if n < 3:
+                spread_bias(nc.vector, row_order[n])
             for r, m in projections[2 * n : 2 * n + 2]:
                 project_chunk(r, m)
-        nc.sync.dma_start(wqkv_sb[:, :, 2 * C : 3 * C], wqkv_blocks[:, :, 2 * C : 3 * C])
         nc.sync.dma_start(wproj_sb[:], wproj.rearrange("(cb p) m -> p cb m", p=PART))
         cq_ps = logit_banks.tile([PART, KEYS], F32, name="cq_ps", tag="e_ps")
         cq_sums = cq_ps[:, 0 : 2 * HEADS * CLOUDS].rearrange("p (b u) -> p b u", u=CLOUDS)
@@ -318,48 +324,56 @@ def tile_serializedattention_b_kernel(tc, feat, cls_tok, wqkv, bqkv, wproj, bpro
                     start=(cb == 0),
                     stop=(cb == C_BLOCKS - 1),
                 )
-        for b, slot in pieces[0:PATCHES_PER_CLOUD]:
-            look_up(b, slot)
         nc.vector.tensor_tensor(
             cq[:], cq_sums, bias[:, HEADS:ROW_BLOCKS].unsqueeze(2).to_broadcast([PART, 2 * HEADS, CLOUDS]), ADD
         )
-        for h in range(HEADS):
-            nc.gpsimd.tensor_copy(cv_cols[:, :, h, h], cq[:, HEADS + h, :])
-        for b, slot in pieces[PATCHES_PER_CLOUD:first_pieces]:
-            look_up(b, slot)
+        look_up_queries_and_keys(0, 0)
+        round_queries_and_keys(0, 0)
         for r, n in projections[2 * CHUNKS : first_projections]:
             project_chunk(r, n)
-        cv_ps = flips.tile([PART, CLOUDS, HEADS, DH], BF16, name="cv_ps", tag="flip_ps")
-        for u in range(CLOUDS):
-            for h in range(HEADS):
-                nc.tensor.transpose(cv_ps[:, u, h, :], cv_cols[:, u, h, :], ident[:])
-        nc.scalar.copy(cv_rows[:], cv_ps[:])
+        nc.vector.tensor_copy(
+            cv_spread[:], cq[:, HEADS : 2 * HEADS, :].unsqueeze(3).to_broadcast([PART, HEADS, CLOUDS, PART])
+        )
+        for first in range(0, HEADS, 2):
+            cv_ps = sums.tile([PART, 2, CLOUDS, DH], F32, name="cv_ps", tag="sum_ps")
+            for i in range(2):
+                for u in range(CLOUDS):
+                    nc.tensor.matmul(
+                        cv_ps[:, i, u, :], lhsT=cv_spread[:, first + i, u, :], rhs=ident[:], start=True, stop=True
+                    )
+            nc.scalar.copy(cv_rows[:, first : first + 2, :, :], cv_ps[:])
 
-        last_lag = 8 + C_BLOCKS - 1
-        for tick in range(len(units) + last_lag + 1):
-            if tick < len(units):
+        out_blocks = [(n, m) for n in range(CHUNKS) for m in range(C_BLOCKS)]
+        first_out = UNITS - PATCHES + PAIR - 1 + 5
+        for tick in range(first_out + len(out_blocks) // 2):
+            if tick < UNITS:
                 logits(tick)
-            if 0 <= tick - 1 < len(units):
+            if 0 <= tick - 1 < UNITS:
                 exponentials(tick - 1)
-            if 0 <= tick - 2 < len(units):
+            if 0 <= tick - 2 < UNITS:
                 divide(tick - 2)
-            for r, n in projections[first_projections + 2 * tick : first_projections + 2 * tick + 2]:
+            if 0 <= tick - 3 < UNITS:
+                copy_flipped(tick - 3)
+            if 0 <= tick - 4 < UNITS and (tick - 4) % PAIR == PAIR - 1:
+                copy_weighted_sums((tick - 4) // PAIR)
+            done = first_projections + (3 * tick + 1) // 2
+            for r, n in projections[done : first_projections + (3 * tick + 4) // 2]:
                 project_chunk(r, n)
-            for b, slot in pieces[first_pieces + 3 * tick : first_pieces + 3 * tick + 3]:
-                look_up(b, slot)
-            if tick < len(units):
+            if tick >= first_out:
+                for n, m in out_blocks[2 * (tick - first_out) : 2 * (tick - first_out) + 2]:
+                    project_out(n, m)
+            piece = tick // 2
+            if tick % 2 == 0 and piece + 1 < HEADS * PIECES:
+                look_up_queries_and_keys(*divmod(piece + 1, PIECES))
+            if tick % 2 == 1 and piece + 1 < HEADS * PIECES:
+                round_queries_and_keys(*divmod(piece + 1, PIECES))
+            if tick % 2 == 1 and piece < HEADS * PIECES:
+                look_up_values(*divmod(piece, PIECES))
+            if tick < UNITS:
                 maxima(tick)
-            if 0 <= tick - 1 < len(units):
+            if 0 <= tick - 1 < UNITS:
                 reciprocals(tick - 1)
-            if 0 <= tick - 3 < len(units) and (tick - 3) % 2 == 1:
-                flip_weights((tick - 3) // 2)
-            if tick - 4 in patch_ending_at:
-                flip_class_weights(patch_ending_at[tick - 4])
-                flip_values(patch_ending_at[tick - 4])
-            if tick - 6 in patch_ending_at:
-                weighted_sums(patch_ending_at[tick - 6], 0)
-            if tick - 7 in patch_ending_at:
-                weighted_sums(patch_ending_at[tick - 7], 2)
-            for m in range(C_BLOCKS):
-                if tick - 8 - m in chunk_ending_at:
-                    project_out(chunk_ending_at[tick - 8 - m], m)
+            if 0 <= tick - 2 < UNITS:
+                flip(tick - 2)
+            if 0 <= tick - 3 < UNITS:
+                weighted_sums(tick - 3)

@@ -30,7 +30,7 @@ ROW_BLOCKS = 3 * C // PART
 CHUNK = 512
 CHUNKS = POINTS // CHUNK
 SLICE = CHUNK // 2
-STAGED = 4
+SLICES = POINTS // SLICE
 HALVES = PATCH // PART
 PAIR = 2
 PIECE = PAIR * PATCH
@@ -50,7 +50,7 @@ def tile_serializedattention_b_kernel(tc, feat, cls_tok, wqkv, bqkv, wproj, bpro
     nc = tc.nc
     with ExitStack() as ctx:
         held = ctx.enter_context(tc.tile_pool(name="held", bufs=1))
-        stage = ctx.enter_context(tc.tile_pool(name="stage", bufs=STAGED))
+        stage = ctx.enter_context(tc.tile_pool(name="stage", bufs=SLICES))
         windows = ctx.enter_context(tc.tile_pool(name="windows", bufs=6))
         picks = ctx.enter_context(tc.tile_pool(name="picks", bufs=2))
         per_head = ctx.enter_context(tc.tile_pool(name="per_head", bufs=2))
@@ -82,16 +82,22 @@ def tile_serializedattention_b_kernel(tc, feat, cls_tok, wqkv, bqkv, wproj, bpro
         def round_slice(s):
             nc.vector.tensor_copy(feat_bf[:, :, s * SLICE : (s + 1) * SLICE], staged_of[s][:])
 
+        def load_wqkv(first_head, heads):
+            for kind in range(3):
+                cols = slice(kind * C + first_head * DH, kind * C + (first_head + heads) * DH)
+                nc.sync.dma_start(wqkv_sb[:, :, cols], wqkv_blocks[:, :, cols])
+
         nc.scalar.dma_start(bias_rows[0:ROW_BLOCKS, :], bqkv.rearrange("(b p) o -> b (p o)", p=PART))
         nc.scalar.dma_start(
             bias_rows[ROW_BLOCKS : ROW_BLOCKS + C_BLOCKS, :], bproj.rearrange("(b p) o -> b (p o)", p=PART)
         )
         nc.scalar.dma_start(cls_sb[:], cls_tok.rearrange("(cb p) u -> p cb u", p=PART))
-        nc.sync.dma_start(wqkv_sb[:, :, 0 : 2 * C], wqkv_blocks[:, :, 0 : 2 * C])
-        for s in range(STAGED):
-            load_slice(s)
-        nc.scalar.dma_start(wqkv_sb[:, :, 2 * C : 3 * C], wqkv_blocks[:, :, 2 * C : 3 * C])
+        load_wqkv(0, 1)
         nc.sync.dma_start(offsets[:], offs)
+        for s in range(SLICES):
+            load_slice(s)
+        load_wqkv(1, HEADS - 1)
+        nc.sync.dma_start(wproj_sb[:], wproj.rearrange("(cb p) m -> p cb m", p=PART))
 
         zero = held.tile([PART, 1], F32, name="zero")
         nc.vector.memset(zero[:], 0.0)
@@ -113,9 +119,8 @@ def tile_serializedattention_b_kernel(tc, feat, cls_tok, wqkv, bqkv, wproj, bpro
             engine.tensor_copy(bias_wide[:, r, :], bias[:, r : r + 1].to_broadcast([PART, PIECE]))
 
         row_order = [r for h in range(HEADS) for r in (h, HEADS + h, 2 * HEADS + h)]
-        projections = [(r, n) for n in range(CHUNKS) for r in row_order[0:2]] + [
-            (r, n) for r in row_order[2:] for n in range(CHUNKS)
-        ]
+        first_projections = [(r, n) for n in range(CHUNKS) for r in row_order[0:2]]
+        projections = [(r, n) for r in row_order[2:] for n in range(0, CHUNKS, 2)]
 
         cq = held.tile([PART, 2 * HEADS, CLOUDS], F32, name="cq")
         cv_spread = held.tile([PART, HEADS, CLOUDS, PART], BF16, name="cv_spread")
@@ -144,6 +149,24 @@ def tile_serializedattention_b_kernel(tc, feat, cls_tok, wqkv, bqkv, wproj, bpro
                     stop=(cb == C_BLOCKS - 1),
                 )
             nc.scalar.copy(window_of[r][:, cols], p_ps[:])
+
+        def project_two_chunks(r, first):
+            if first == 0:
+                window_of[r] = windows.tile([PART, POINTS], F32, name="window")
+            banks = [sums.tile([PART, CHUNK], F32, name="p_ps", tag="sum_ps") for n in range(2)]
+            for cb in range(C_BLOCKS):
+                for i in range(2):
+                    n = first + i
+                    nc.tensor.matmul(
+                        banks[i][:],
+                        lhsT=wqkv_sb[:, cb, r * PART : (r + 1) * PART],
+                        rhs=feat_bf[:, cb, n * CHUNK : (n + 1) * CHUNK],
+                        start=(cb == 0),
+                        stop=(cb == C_BLOCKS - 1),
+                    )
+            for i in range(2):
+                n = first + i
+                nc.scalar.copy(window_of[r][:, n * CHUNK : (n + 1) * CHUNK], banks[i][:])
 
         def look_up(dest, r, g):
             nc.vector.tensor_tensor(
@@ -176,6 +199,31 @@ def tile_serializedattention_b_kernel(tc, feat, cls_tok, wqkv, bqkv, wproj, bpro
             picked_v = picks.tile([PART, PIECE], F32, name="picked_v")
             look_up(picked_v[:], 2 * HEADS + h, g)
             nc.vector.tensor_copy(v_of[h][:, g * PIECE : (g + 1) * PIECE], picked_v[:])
+
+        def project_class_tokens(first_head, heads):
+            cq_ps = logit_banks.tile([PART, KEYS], F32, name="cq_ps", tag="e_ps")
+            cq_sums = cq_ps[:, 0 : 2 * heads * CLOUDS].rearrange("p (k h u) -> p k h u", k=2, u=CLOUDS)
+            for kind in range(2):
+                for i in range(heads):
+                    r = (1 + kind) * HEADS + first_head + i
+                    for cb in range(C_BLOCKS):
+                        nc.tensor.matmul(
+                            cq_sums[:, kind, i, :],
+                            lhsT=wqkv_sb[:, cb, r * PART : (r + 1) * PART],
+                            rhs=cls_sb[:, cb, :],
+                            start=(cb == 0),
+                            stop=(cb == C_BLOCKS - 1),
+                        )
+            these = slice(first_head, first_head + heads)
+            nc.vector.tensor_tensor(
+                cq[:].rearrange("p (k h) u -> p k h u", k=2)[:, :, these, :],
+                cq_sums,
+                bias[:, HEADS:ROW_BLOCKS]
+                .rearrange("p (k h) -> p k h", k=2)[:, :, these]
+                .unsqueeze(3)
+                .to_broadcast([PART, 2, heads, CLOUDS]),
+                ADD,
+            )
 
         def logits(i):
             h, t = divmod(i, PATCHES)
@@ -263,18 +311,21 @@ def tile_serializedattention_b_kernel(tc, feat, cls_tok, wqkv, bqkv, wproj, bpro
             if place == 0:
                 att_ps_of[pair] = att_banks.tile([PART, PIECE], F32, name="att_ps")
             att_ps = att_ps_of[pair]
-            for jb in range(HALVES):
-                queries = slice(place * PATCH + jb * PART, place * PATCH + (jb + 1) * PART)
-                for ib in range(HALVES):
-                    nc.tensor.matmul(
-                        att_ps[:, queries],
-                        lhsT=flipped_of[i][:, HALVES * PATCH + ib * DH : HALVES * PATCH + (ib + 1) * DH],
-                        rhs=flipped_of[i][:, ib * PATCH + jb * PART : ib * PATCH + (jb + 1) * PART],
-                        start=(ib == 0),
-                        stop=False,
-                    )
+            for ib in range(HALVES):
                 nc.tensor.matmul(
-                    att_ps[:, queries], lhsT=cv_rows[:, h, u, :], rhs=diag_of[i][:, jb, :], start=False, stop=True
+                    att_ps[:, place * PATCH : (place + 1) * PATCH],
+                    lhsT=flipped_of[i][:, HALVES * PATCH + ib * DH : HALVES * PATCH + (ib + 1) * DH],
+                    rhs=flipped_of[i][:, ib * PATCH : (ib + 1) * PATCH],
+                    start=(ib == 0),
+                    stop=False,
+                )
+            for jb in range(HALVES):
+                nc.tensor.matmul(
+                    att_ps[:, place * PATCH + jb * PART : place * PATCH + (jb + 1) * PART],
+                    lhsT=cv_rows[:, h, u, :],
+                    rhs=diag_of[i][:, jb, :],
+                    start=False,
+                    stop=(jb == HALVES - 1),
                 )
 
         def copy_weighted_sums(pair):
@@ -300,37 +351,22 @@ def tile_serializedattention_b_kernel(tc, feat, cls_tok, wqkv, bqkv, wproj, bpro
                 nc.vector.tensor_scalar(out=out_sb[:], in0=out_ps[:], scalar1=bproj_m, scalar2=None, op0=ADD)
             nc.sync.dma_start(out[m * PART : (m + 1) * PART, cols], out_sb[:])
 
-        first_projections = 3 * CHUNKS
+        project_class_tokens(0, 1)
         for r in row_order[3:]:
             spread_bias(nc.gpsimd, r)
         for n in range(CHUNKS):
             for s in (2 * n, 2 * n + 1):
                 round_slice(s)
-                if s + STAGED < POINTS // SLICE:
-                    load_slice(s + STAGED)
             if n < 3:
                 spread_bias(nc.vector, row_order[n])
-            for r, m in projections[2 * n : 2 * n + 2]:
+            for r, m in first_projections[2 * n : 2 * n + 2]:
                 project_chunk(r, m)
-        nc.sync.dma_start(wproj_sb[:], wproj.rearrange("(cb p) m -> p cb m", p=PART))
-        cq_ps = logit_banks.tile([PART, KEYS], F32, name="cq_ps", tag="e_ps")
-        cq_sums = cq_ps[:, 0 : 2 * HEADS * CLOUDS].rearrange("p (b u) -> p b u", u=CLOUDS)
-        for g in range(2 * HEADS):
-            for cb in range(C_BLOCKS):
-                nc.tensor.matmul(
-                    cq_sums[:, g, :],
-                    lhsT=wqkv_sb[:, cb, (HEADS + g) * PART : (HEADS + g + 1) * PART],
-                    rhs=cls_sb[:, cb, :],
-                    start=(cb == 0),
-                    stop=(cb == C_BLOCKS - 1),
-                )
-        nc.vector.tensor_tensor(
-            cq[:], cq_sums, bias[:, HEADS:ROW_BLOCKS].unsqueeze(2).to_broadcast([PART, 2 * HEADS, CLOUDS]), ADD
-        )
         look_up_queries_and_keys(0, 0)
         round_queries_and_keys(0, 0)
-        for r, n in projections[2 * CHUNKS : first_projections]:
-            project_chunk(r, n)
+        early = 2
+        for r, n in projections[0:early]:
+            project_two_chunks(r, n)
+        project_class_tokens(1, HEADS - 1)
         nc.vector.tensor_copy(
             cv_spread[:], cq[:, HEADS : 2 * HEADS, :].unsqueeze(3).to_broadcast([PART, HEADS, CLOUDS, PART])
         )
@@ -356,9 +392,8 @@ def tile_serializedattention_b_kernel(tc, feat, cls_tok, wqkv, bqkv, wproj, bpro
                 copy_flipped(tick - 3)
             if 0 <= tick - 4 < UNITS and (tick - 4) % PAIR == PAIR - 1:
                 copy_weighted_sums((tick - 4) // PAIR)
-            done = first_projections + (3 * tick + 1) // 2
-            for r, n in projections[done : first_projections + (3 * tick + 4) // 2]:
-                project_chunk(r, n)
+            for r, n in projections[early + (3 * tick + 1) // 4 : early + (3 * tick + 4) // 4]:
+                project_two_chunks(r, n)
             if tick >= first_out:
                 for n, m in out_blocks[2 * (tick - first_out) : 2 * (tick - first_out) + 2]:
                     project_out(n, m)

@@ -198,7 +198,7 @@ def tile_serializedattention_b_kernel(tc, feat, cls_tok, wqkv, bqkv, wproj, bpro
                 v_of[h] = per_head.tile([PART, POINTS], BF16, name="v_bf")
             picked_v = picks.tile([PART, PIECE], F32, name="picked_v")
             look_up(picked_v[:], 2 * HEADS + h, g)
-            nc.vector.tensor_copy(v_of[h][:, g * PIECE : (g + 1) * PIECE], picked_v[:])
+            nc.scalar.copy(v_of[h][:, g * PIECE : (g + 1) * PIECE], picked_v[:])
 
         def project_class_tokens(first_head, heads):
             cq_ps = logit_banks.tile([PART, KEYS], F32, name="cq_ps", tag="e_ps")

@@ -115,8 +115,8 @@ def tile_serializedattention_b_kernel(tc, feat, cls_tok, wqkv, bqkv, wproj, bpro
         nc.vector.tensor_copy(bias[:], bias_ps[:, 0 : ROW_BLOCKS + C_BLOCKS])
         bias_wide = held.tile([PART, ROW_BLOCKS, PIECE], F32, name="bias_wide")
 
-        def spread_bias(engine, r):
-            engine.tensor_copy(bias_wide[:, r, :], bias[:, r : r + 1].to_broadcast([PART, PIECE]))
+        def spread_bias(r):
+            nc.vector.tensor_copy(bias_wide[:, r, :], bias[:, r : r + 1].to_broadcast([PART, PIECE]))
 
         row_order = [r for h in range(HEADS) for r in (h, HEADS + h, 2 * HEADS + h)]
         first_projections = [(r, n) for n in range(CHUNKS) for r in row_order[0:2]]
@@ -352,13 +352,11 @@ def tile_serializedattention_b_kernel(tc, feat, cls_tok, wqkv, bqkv, wproj, bpro
             nc.sync.dma_start(out[m * PART : (m + 1) * PART, cols], out_sb[:])
 
         project_class_tokens(0, 1)
-        for r in row_order[3:]:
-            spread_bias(nc.gpsimd, r)
         for n in range(CHUNKS):
             for s in (2 * n, 2 * n + 1):
                 round_slice(s)
-            if n < 3:
-                spread_bias(nc.vector, row_order[n])
+            for r in row_order[3 * n : 3 * n + 3]:
+                spread_bias(r)
             for r, m in first_projections[2 * n : 2 * n + 2]:
                 project_chunk(r, m)
         look_up_queries_and_keys(0, 0)

@@ -36,7 +36,7 @@ PAIR = 2
 PIECE = PAIR * PATCH
 PIECES = POINTS // PIECE
 OFFSET_COLS = PIECE // 16
-SCALE = DH**-0.5
+ROOT_SCALE = DH**-0.25
 
 FLOPS = (
     2 * C * 3 * C * POINTS
@@ -179,18 +179,24 @@ def tile_serializedattention_b_kernel(tc, feat, cls_tok, wqkv, bqkv, wproj, bpro
         def look_up_queries_and_keys(h, g):
             if g == 0:
                 qk_of[h] = per_head.tile([PART, 2, PATCHES, KEY_PITCH], BF16, name="qk_bf")
-                nc.vector.tensor_copy(
-                    qk_of[h][:, 1, :, PATCH:KEYS].rearrange("p (u t) o -> p u (t o)", u=CLOUDS),
-                    cq[:, h, :].unsqueeze(2).to_broadcast([PART, CLOUDS, PATCHES_PER_CLOUD]),
+                nc.vector.tensor_scalar(
+                    out=qk_of[h][:, 1, :, PATCH:KEYS].rearrange("p (u t) o -> p u (t o)", u=CLOUDS),
+                    in0=cq[:, h, :].unsqueeze(2).to_broadcast([PART, CLOUDS, PATCHES_PER_CLOUD]),
+                    scalar1=ROOT_SCALE,
+                    scalar2=None,
+                    op0=MULT,
                 )
             picked_qk_of[(h, g)] = picks.tile([PART, 2, PIECE], F32, name="picked_qk")
             look_up(picked_qk_of[(h, g)][:, 0, :], h, g)
             look_up(picked_qk_of[(h, g)][:, 1, :], HEADS + h, g)
 
         def round_queries_and_keys(h, g):
-            nc.vector.tensor_copy(
-                qk_of[h][:, :, g * PAIR : (g + 1) * PAIR, 0:PATCH],
-                picked_qk_of[(h, g)][:].rearrange("p a (t j) -> p a t j", t=PAIR),
+            nc.vector.tensor_scalar(
+                out=qk_of[h][:, :, g * PAIR : (g + 1) * PAIR, 0:PATCH],
+                in0=picked_qk_of[(h, g)][:].rearrange("p a (t j) -> p a t j", t=PAIR),
+                scalar1=ROOT_SCALE,
+                scalar2=None,
+                op0=MULT,
             )
 
         def look_up_values(h, g):
@@ -240,11 +246,11 @@ def tile_serializedattention_b_kernel(tc, feat, cls_tok, wqkv, bqkv, wproj, bpro
                 e_of[i].append(e_ps)
 
         def maxima(i):
-            top = stats.tile([PART, HALVES], F32, name="top")
-            for jb in range(HALVES):
-                nc.vector.reduce_max(out=top[:, jb : jb + 1], in_=e_of[i][jb][:], axis=ALONG_FREE)
             shift_of[i] = stats.tile([PART, HALVES], F32, name="shift")
-            nc.vector.tensor_scalar(out=shift_of[i][:], in0=top[:], scalar1=-SCALE, scalar2=None, op0=MULT)
+            for jb in range(HALVES):
+                nc.vector.reduce_max(
+                    out=shift_of[i][:, jb : jb + 1], in_=e_of[i][jb][:], axis=ALONG_FREE, negate=True
+                )
 
         def exponentials(i):
             total_of[i] = stats.tile([PART, HALVES], F32, name="total")
@@ -256,7 +262,6 @@ def tile_serializedattention_b_kernel(tc, feat, cls_tok, wqkv, bqkv, wproj, bpro
                     in_=e_of[i][jb][:],
                     func=EXP,
                     bias=shift_of[i][:, jb : jb + 1],
-                    scale=SCALE,
                     accum_out=total_of[i][:, jb : jb + 1],
                 )
                 ex_of[i].append(ex)

@@ -52,11 +52,11 @@ def tile_serializedattention_b_kernel(tc, feat, cls_tok, wqkv, bqkv, wproj, bpro
         held = ctx.enter_context(tc.tile_pool(name="held", bufs=1))
         stage = ctx.enter_context(tc.tile_pool(name="stage", bufs=SLICES))
         windows = ctx.enter_context(tc.tile_pool(name="windows", bufs=6))
-        picks = ctx.enter_context(tc.tile_pool(name="picks", bufs=2))
+        picks = ctx.enter_context(tc.tile_pool(name="picks", bufs=3))
         per_head = ctx.enter_context(tc.tile_pool(name="per_head", bufs=2))
-        stats = ctx.enter_context(tc.tile_pool(name="stats", bufs=8))
-        exps = ctx.enter_context(tc.tile_pool(name="exps", bufs=6))
-        per_unit = ctx.enter_context(tc.tile_pool(name="per_unit", bufs=3))
+        stats = ctx.enter_context(tc.tile_pool(name="stats", bufs=12))
+        exps = ctx.enter_context(tc.tile_pool(name="exps", bufs=8))
+        per_unit = ctx.enter_context(tc.tile_pool(name="per_unit", bufs=5))
         diagonals = ctx.enter_context(tc.tile_pool(name="diagonals", bufs=6))
         results = ctx.enter_context(tc.tile_pool(name="results", bufs=4))
         sums = ctx.enter_context(tc.psum_pool(name="sums", bufs=2))

@@ -35,7 +35,7 @@ HALVES = PATCH // PART
 PAIR = 2
 PIECE = PAIR * PATCH
 PIECES = POINTS // PIECE
-OFFSET_COLS = PIECE // 16
+OFFSET_COLS = PATCH // 16
 ROOT_SCALE = DH**-0.25
 
 FLOPS = (
@@ -50,8 +50,7 @@ def tile_serializedattention_b_kernel(tc, feat, cls_tok, wqkv, bqkv, wproj, bpro
     nc = tc.nc
     with ExitStack() as ctx:
         held = ctx.enter_context(tc.tile_pool(name="held", bufs=1))
-        stage = ctx.enter_context(tc.tile_pool(name="stage", bufs=SLICES))
-        windows = ctx.enter_context(tc.tile_pool(name="windows", bufs=6))
+        windows = ctx.enter_context(tc.tile_pool(name="windows", bufs=8))
         picks = ctx.enter_context(tc.tile_pool(name="picks", bufs=3))
         per_head = ctx.enter_context(tc.tile_pool(name="per_head", bufs=2))
         stats = ctx.enter_context(tc.tile_pool(name="stats", bufs=12))
@@ -76,27 +75,36 @@ def tile_serializedattention_b_kernel(tc, feat, cls_tok, wqkv, bqkv, wproj, bpro
         staged_of = {}
 
         def load_slice(s):
-            staged_of[s] = stage.tile([PART, C_BLOCKS, SLICE], F32, name="staged")
-            nc.sync.dma_start(staged_of[s][:], feat_blocks[:, :, s * SLICE : (s + 1) * SLICE])
+            n, half = divmod(s, CHUNK // SLICE)
+            if half == 0:
+                staged_of[n] = windows.tile([PART, C_BLOCKS, CHUNK], F32, name="staged", tag="window")
+            nc.sync.dma_start(
+                staged_of[n][:, :, half * SLICE : (half + 1) * SLICE], feat_blocks[:, :, s * SLICE : (s + 1) * SLICE]
+            )
 
         def round_slice(s):
-            nc.vector.tensor_copy(feat_bf[:, :, s * SLICE : (s + 1) * SLICE], staged_of[s][:])
+            n, half = divmod(s, CHUNK // SLICE)
+            nc.vector.tensor_copy(
+                feat_bf[:, :, s * SLICE : (s + 1) * SLICE], staged_of[n][:, :, half * SLICE : (half + 1) * SLICE]
+            )
 
-        def load_wqkv(first_head, heads):
-            for kind in range(3):
-                cols = slice(kind * C + first_head * DH, kind * C + (first_head + heads) * DH)
-                nc.sync.dma_start(wqkv_sb[:, :, cols], wqkv_blocks[:, :, cols])
+        def load_wqkv(kind, first_head, heads):
+            cols = slice(kind * C + first_head * DH, kind * C + (first_head + heads) * DH)
+            nc.sync.dma_start(wqkv_sb[:, :, cols], wqkv_blocks[:, :, cols])
 
         nc.scalar.dma_start(bias_rows[0:ROW_BLOCKS, :], bqkv.rearrange("(b p) o -> b (p o)", p=PART))
         nc.scalar.dma_start(
             bias_rows[ROW_BLOCKS : ROW_BLOCKS + C_BLOCKS, :], bproj.rearrange("(b p) o -> b (p o)", p=PART)
         )
         nc.scalar.dma_start(cls_sb[:], cls_tok.rearrange("(cb p) u -> p cb u", p=PART))
-        load_wqkv(0, 1)
+        load_wqkv(0, 0, 1)
+        load_wqkv(1, 0, 1)
         nc.sync.dma_start(offsets[:], offs)
         for s in range(SLICES):
             load_slice(s)
-        load_wqkv(1, HEADS - 1)
+        load_wqkv(2, 0, 1)
+        for kind in range(3):
+            load_wqkv(kind, 1, HEADS - 1)
         nc.sync.dma_start(wproj_sb[:], wproj.rearrange("(cb p) m -> p cb m", p=PART))
 
         zero = held.tile([PART, 1], F32, name="zero")
@@ -118,8 +126,9 @@ def tile_serializedattention_b_kernel(tc, feat, cls_tok, wqkv, bqkv, wproj, bpro
         def spread_bias(r):
             nc.vector.tensor_copy(bias_wide[:, r, :], bias[:, r : r + 1].to_broadcast([PART, PIECE]))
 
+        pieces = [(h, g) for h in range(HEADS) for g in range(PIECES)]
+        units = [(h, PAIR * g + k) for h, g in pieces for k in range(PAIR)]
         row_order = [r for h in range(HEADS) for r in (h, HEADS + h, 2 * HEADS + h)]
-        first_projections = [(r, n) for n in range(CHUNKS) for r in row_order[0:2]]
         projections = [(r, n) for r in row_order[2:] for n in range(0, CHUNKS, 2)]
 
         cq = held.tile([PART, 2 * HEADS, CLOUDS], F32, name="cq")
@@ -135,11 +144,14 @@ def tile_serializedattention_b_kernel(tc, feat, cls_tok, wqkv, bqkv, wproj, bpro
         flip_ps_of, flipped_of = {}, {}
         att_ps_of = {}
 
-        def project_chunk(r, n):
-            if n == 0:
+        def project_slice(r, s):
+            if s == 0:
                 window_of[r] = windows.tile([PART, POINTS], F32, name="window")
-            cols = slice(n * CHUNK, (n + 1) * CHUNK)
-            p_ps = sums.tile([PART, CHUNK], F32, name="p_ps", tag="sum_ps")
+            cols = slice(s * SLICE, (s + 1) * SLICE)
+            if r < HEADS:
+                p_ps = sums.tile([PART, SLICE], F32, name="p_ps", tag="sum_ps")
+            else:
+                p_ps = logit_banks.tile([PART, SLICE], F32, name="p_ps", tag="e_ps")
             for cb in range(C_BLOCKS):
                 nc.tensor.matmul(
                     p_ps[:],
@@ -168,17 +180,30 @@ def tile_serializedattention_b_kernel(tc, feat, cls_tok, wqkv, bqkv, wproj, bpro
                 n = first + i
                 nc.scalar.copy(window_of[r][:, n * CHUNK : (n + 1) * CHUNK], banks[i][:])
 
-        def look_up(dest, r, g):
+        def look_up(dest, r, t, patches):
             nc.vector.tensor_tensor(
                 dest,
-                window_of[r][:].indirect(offsets[:, g * OFFSET_COLS : (g + 1) * OFFSET_COLS]),
-                bias_wide[:, r, :],
+                window_of[r][:].indirect(offsets[:, t * OFFSET_COLS : (t + patches) * OFFSET_COLS]),
+                bias_wide[:, r, 0 : patches * PATCH],
                 ADD,
             )
 
-        def look_up_queries_and_keys(h, g):
-            if g == 0:
+        def look_up_queries_and_keys(h, t, patches):
+            if t == 0:
                 qk_of[h] = per_head.tile([PART, 2, PATCHES, KEY_PITCH], BF16, name="qk_bf")
+            picked_qk_of[(h, t)] = picks.tile([PART, 2, PIECE], F32, name="picked_qk")
+            for a in range(2):
+                look_up(picked_qk_of[(h, t)][:, a, 0 : patches * PATCH], a * HEADS + h, t, patches)
+
+        def round_queries_and_keys(h, t, patches):
+            nc.vector.tensor_scalar(
+                out=qk_of[h][:, :, t : t + patches, 0:PATCH],
+                in0=picked_qk_of[(h, t)][:, :, 0 : patches * PATCH].rearrange("p a (t j) -> p a t j", t=patches),
+                scalar1=ROOT_SCALE,
+                scalar2=None,
+                op0=MULT,
+            )
+            if t == 0:
                 nc.vector.tensor_scalar(
                     out=qk_of[h][:, 1, :, PATCH:KEYS].rearrange("p (u t) o -> p u (t o)", u=CLOUDS),
                     in0=cq[:, h, :].unsqueeze(2).to_broadcast([PART, CLOUDS, PATCHES_PER_CLOUD]),
@@ -186,53 +211,45 @@ def tile_serializedattention_b_kernel(tc, feat, cls_tok, wqkv, bqkv, wproj, bpro
                     scalar2=None,
                     op0=MULT,
                 )
-            picked_qk_of[(h, g)] = picks.tile([PART, 2, PIECE], F32, name="picked_qk")
-            look_up(picked_qk_of[(h, g)][:, 0, :], h, g)
-            look_up(picked_qk_of[(h, g)][:, 1, :], HEADS + h, g)
-
-        def round_queries_and_keys(h, g):
-            nc.vector.tensor_scalar(
-                out=qk_of[h][:, :, g * PAIR : (g + 1) * PAIR, 0:PATCH],
-                in0=picked_qk_of[(h, g)][:].rearrange("p a (t j) -> p a t j", t=PAIR),
-                scalar1=ROOT_SCALE,
-                scalar2=None,
-                op0=MULT,
-            )
 
         def look_up_values(h, g):
             if g == 0:
                 v_of[h] = per_head.tile([PART, POINTS], BF16, name="v_bf")
             picked_v = picks.tile([PART, PIECE], F32, name="picked_v")
-            look_up(picked_v[:], 2 * HEADS + h, g)
+            look_up(picked_v[:], 2 * HEADS + h, g * PAIR, PAIR)
             nc.scalar.copy(v_of[h][:, g * PIECE : (g + 1) * PIECE], picked_v[:])
 
-        def project_class_tokens(first_head, heads):
-            cq_ps = logit_banks.tile([PART, KEYS], F32, name="cq_ps", tag="e_ps")
-            cq_sums = cq_ps[:, 0 : 2 * heads * CLOUDS].rearrange("p (k h u) -> p k h u", k=2, u=CLOUDS)
+        def class_tokens(h):
+            cq_ps = sums.tile([PART, 2, CLOUDS], F32, name="cq_ps", tag="sum_ps")
             for kind in range(2):
-                for i in range(heads):
-                    r = (1 + kind) * HEADS + first_head + i
-                    for cb in range(C_BLOCKS):
-                        nc.tensor.matmul(
-                            cq_sums[:, kind, i, :],
-                            lhsT=wqkv_sb[:, cb, r * PART : (r + 1) * PART],
-                            rhs=cls_sb[:, cb, :],
-                            start=(cb == 0),
-                            stop=(cb == C_BLOCKS - 1),
-                        )
-            these = slice(first_head, first_head + heads)
+                r = (1 + kind) * HEADS + h
+                for cb in range(C_BLOCKS):
+                    nc.tensor.matmul(
+                        cq_ps[:, kind, :],
+                        lhsT=wqkv_sb[:, cb, r * PART : (r + 1) * PART],
+                        rhs=cls_sb[:, cb, :],
+                        start=(cb == 0),
+                        stop=(cb == C_BLOCKS - 1),
+                    )
             nc.vector.tensor_tensor(
-                cq[:].rearrange("p (k h) u -> p k h u", k=2)[:, :, these, :],
-                cq_sums,
+                cq[:].rearrange("p (k h) u -> p k h u", k=2)[:, :, h, :],
+                cq_ps[:],
                 bias[:, HEADS:ROW_BLOCKS]
-                .rearrange("p (k h) -> p k h", k=2)[:, :, these]
-                .unsqueeze(3)
-                .to_broadcast([PART, 2, heads, CLOUDS]),
+                .rearrange("p (k h) -> p k h", k=2)[:, :, h]
+                .unsqueeze(2)
+                .to_broadcast([PART, 2, CLOUDS]),
                 ADD,
             )
+            nc.vector.tensor_copy(cv_spread[:, h, :, :], cq[:, HEADS + h, :].unsqueeze(2).to_broadcast([PART, CLOUDS, PART]))
+
+        def class_value_rows(h):
+            cv_ps = sums.tile([PART, CLOUDS, DH], F32, name="cv_ps", tag="sum_ps")
+            for u in range(CLOUDS):
+                nc.tensor.matmul(cv_ps[:, u, :], lhsT=cv_spread[:, h, u, :], rhs=ident[:], start=True, stop=True)
+            nc.scalar.copy(cv_rows[:, h, :, :], cv_ps[:])
 
         def logits(i):
-            h, t = divmod(i, PATCHES)
+            h, t = units[i]
             e_of[i] = []
             for jb in range(HALVES):
                 e_ps = logit_banks.tile([PART, KEYS], F32, name="e_ps")
@@ -288,7 +305,7 @@ def tile_serializedattention_b_kernel(tc, feat, cls_tok, wqkv, bqkv, wproj, bpro
                 )
 
         def flip(i):
-            h, t = divmod(i, PATCHES)
+            h, t = units[i]
             flip_ps = flips.tile([PART, HALVES * (PATCH + DH)], BF16, name="flip_ps")
             for ib in range(HALVES):
                 for jb in range(HALVES):
@@ -310,7 +327,7 @@ def tile_serializedattention_b_kernel(tc, feat, cls_tok, wqkv, bqkv, wproj, bpro
             nc.scalar.copy(flipped_of[i][:], flip_ps_of[i][:])
 
         def weighted_sums(i):
-            h, t = divmod(i, PATCHES)
+            h, t = units[i]
             u = t // PATCHES_PER_CLOUD
             pair, place = divmod(i, PAIR)
             if place == 0:
@@ -324,17 +341,16 @@ def tile_serializedattention_b_kernel(tc, feat, cls_tok, wqkv, bqkv, wproj, bpro
                     start=(ib == 0),
                     stop=False,
                 )
-            for jb in range(HALVES):
-                nc.tensor.matmul(
-                    att_ps[:, place * PATCH + jb * PART : place * PATCH + (jb + 1) * PART],
-                    lhsT=cv_rows[:, h, u, :],
-                    rhs=diag_of[i][:, jb, :],
-                    start=False,
-                    stop=(jb == HALVES - 1),
-                )
+            nc.tensor.matmul(
+                att_ps[:, place * PATCH : (place + 1) * PATCH],
+                lhsT=cv_rows[:, h, u, :],
+                rhs=diag_of[i][:].rearrange("p b j -> p (b j)"),
+                start=False,
+                stop=True,
+            )
 
         def copy_weighted_sums(pair):
-            h, g = divmod(pair, PIECES)
+            h, g = pieces[pair]
             nc.scalar.copy(att_bf[:, h, g * PIECE : (g + 1) * PIECE], att_ps_of[pair][:])
 
         def project_out(n, m):
@@ -356,35 +372,31 @@ def tile_serializedattention_b_kernel(tc, feat, cls_tok, wqkv, bqkv, wproj, bpro
                 nc.vector.tensor_scalar(out=out_sb[:], in0=out_ps[:], scalar1=bproj_m, scalar2=None, op0=ADD)
             nc.sync.dma_start(out[m * PART : (m + 1) * PART, cols], out_sb[:])
 
-        project_class_tokens(0, 1)
-        for n in range(CHUNKS):
-            for s in (2 * n, 2 * n + 1):
-                round_slice(s)
-            for r in row_order[3 * n : 3 * n + 3]:
-                spread_bias(r)
-            for r, m in first_projections[2 * n : 2 * n + 2]:
-                project_chunk(r, m)
-        look_up_queries_and_keys(0, 0)
-        round_queries_and_keys(0, 0)
+        for s in range(SLICES):
+            round_slice(s)
+            if s % 2 == 0:
+                for r in row_order[3 * s // 2 : 3 * s // 2 + 3]:
+                    spread_bias(r)
+            for r in row_order[0:2]:
+                project_slice(r, s)
+        class_tokens(0)
+        for t in range(PAIR):
+            look_up_queries_and_keys(0, t, 1)
+            round_queries_and_keys(0, t, 1)
         early = 2
         for r, n in projections[0:early]:
             project_two_chunks(r, n)
-        project_class_tokens(1, HEADS - 1)
-        nc.vector.tensor_copy(
-            cv_spread[:], cq[:, HEADS : 2 * HEADS, :].unsqueeze(3).to_broadcast([PART, HEADS, CLOUDS, PART])
-        )
-        for first in range(0, HEADS, 2):
-            cv_ps = sums.tile([PART, 2, CLOUDS, DH], F32, name="cv_ps", tag="sum_ps")
-            for i in range(2):
-                for u in range(CLOUDS):
-                    nc.tensor.matmul(
-                        cv_ps[:, i, u, :], lhsT=cv_spread[:, first + i, u, :], rhs=ident[:], start=True, stop=True
-                    )
-            nc.scalar.copy(cv_rows[:, first : first + 2, :, :], cv_ps[:])
 
-        out_blocks = [(n, m) for n in range(CHUNKS) for m in range(C_BLOCKS)]
-        first_out = UNITS - PATCHES + PAIR - 1 + 5
-        for tick in range(first_out + len(out_blocks) // 2):
+        out_blocks_of = {}
+        for n in range(CHUNKS):
+            for m in range(C_BLOCKS):
+                tick = PAIR * pieces.index((HEADS - 1, n)) + PAIR - 1 + 5 + m // 2
+                out_blocks_of.setdefault(tick, []).append((n, m))
+        for tick in range(max(out_blocks_of) + 1):
+            if 1 <= tick < HEADS:
+                class_tokens(tick)
+            if 0 <= tick - 1 < HEADS:
+                class_value_rows(tick - 1)
             if tick < UNITS:
                 logits(tick)
             if 0 <= tick - 1 < UNITS:
@@ -397,16 +409,17 @@ def tile_serializedattention_b_kernel(tc, feat, cls_tok, wqkv, bqkv, wproj, bpro
                 copy_weighted_sums((tick - 4) // PAIR)
             for r, n in projections[early + (3 * tick + 1) // 4 : early + (3 * tick + 4) // 4]:
                 project_two_chunks(r, n)
-            if tick >= first_out:
-                for n, m in out_blocks[2 * (tick - first_out) : 2 * (tick - first_out) + 2]:
-                    project_out(n, m)
+            for n, m in out_blocks_of.get(tick, []):
+                project_out(n, m)
             piece = tick // 2
             if tick % 2 == 0 and piece + 1 < HEADS * PIECES:
-                look_up_queries_and_keys(*divmod(piece + 1, PIECES))
+                h, g = pieces[piece + 1]
+                look_up_queries_and_keys(h, g * PAIR, PAIR)
             if tick % 2 == 1 and piece + 1 < HEADS * PIECES:
-                round_queries_and_keys(*divmod(piece + 1, PIECES))
+                h, g = pieces[piece + 1]
+                round_queries_and_keys(h, g * PAIR, PAIR)
             if tick % 2 == 1 and piece < HEADS * PIECES:
-                look_up_values(*divmod(piece, PIECES))
+                look_up_values(*pieces[piece])
             if tick < UNITS:
                 maxima(tick)
             if 0 <= tick - 1 < UNITS:

@@ -36,6 +36,7 @@ PAIR = 2
 PIECE = PAIR * PATCH
 PIECES = POINTS // PIECE
 OFFSET_COLS = PATCH // 16
+PACE = 15
 ROOT_SCALE = DH**-0.25
 
 FLOPS = (
@@ -51,17 +52,17 @@ def tile_serializedattention_b_kernel(tc, feat, cls_tok, wqkv, bqkv, wproj, bpro
     with ExitStack() as ctx:
         held = ctx.enter_context(tc.tile_pool(name="held", bufs=1))
         windows = ctx.enter_context(tc.tile_pool(name="windows", bufs=8))
-        picks = ctx.enter_context(tc.tile_pool(name="picks", bufs=3))
+        picks = ctx.enter_context(tc.tile_pool(name="picks", bufs=1))
         per_head = ctx.enter_context(tc.tile_pool(name="per_head", bufs=2))
+        per_pair = ctx.enter_context(tc.tile_pool(name="per_pair", bufs=1))
         stats = ctx.enter_context(tc.tile_pool(name="stats", bufs=12))
         exps = ctx.enter_context(tc.tile_pool(name="exps", bufs=8))
-        per_unit = ctx.enter_context(tc.tile_pool(name="per_unit", bufs=5))
+        per_unit = ctx.enter_context(tc.tile_pool(name="per_unit", bufs=6))
         diagonals = ctx.enter_context(tc.tile_pool(name="diagonals", bufs=6))
         results = ctx.enter_context(tc.tile_pool(name="results", bufs=4))
-        sums = ctx.enter_context(tc.psum_pool(name="sums", bufs=2))
+        sums = ctx.enter_context(tc.psum_pool(name="sums", bufs=3))
         logit_banks = ctx.enter_context(tc.psum_pool(name="logit_banks", bufs=4))
         flips = ctx.enter_context(tc.psum_pool(name="flips", bufs=1))
-        att_banks = ctx.enter_context(tc.psum_pool(name="att_banks", bufs=1))
 
         offsets = held.tile([PART, POINTS // 16], U16, name="offsets")
         wqkv_sb = held.tile([PART, C_BLOCKS, 3 * C], BF16, name="wqkv_sb")
@@ -126,7 +127,8 @@ def tile_serializedattention_b_kernel(tc, feat, cls_tok, wqkv, bqkv, wproj, bpro
         def spread_bias(r):
             nc.vector.tensor_copy(bias_wide[:, r, :], bias[:, r : r + 1].to_broadcast([PART, PIECE]))
 
-        pieces = [(h, g) for h in range(HEADS) for g in range(PIECES)]
+        begins = (0, PIECES, 2 * PIECES, 2 * PIECES + 1)
+        pieces = sorted([(h, g) for h in range(HEADS) for g in range(PIECES)], key=lambda hg: begins[hg[0]] + hg[1])
         units = [(h, PAIR * g + k) for h, g in pieces for k in range(PAIR)]
         row_order = [r for h in range(HEADS) for r in (h, HEADS + h, 2 * HEADS + h)]
         projections = [(r, n) for r in row_order[2:] for n in range(0, CHUNKS, 2)]
@@ -138,10 +140,12 @@ def tile_serializedattention_b_kernel(tc, feat, cls_tok, wqkv, bqkv, wproj, bpro
 
         window_of = {}
         picked_qk_of = {}
-        qk_of, v_of = {}, {}
+        qk_of = {}
+        v_of = {}
         e_of, shift_of, ex_of, total_of, recip_of = {}, {}, {}, {}, {}
         w_of, diag_of = {}, {}
         flip_ps_of, flipped_of = {}, {}
+        out_ps_of = {}
         att_ps_of = {}
 
         def project_slice(r, s):
@@ -189,24 +193,25 @@ def tile_serializedattention_b_kernel(tc, feat, cls_tok, wqkv, bqkv, wproj, bpro
             )
 
         def look_up_queries_and_keys(h, t, patches):
-            if t == 0:
-                qk_of[h] = per_head.tile([PART, 2, PATCHES, KEY_PITCH], BF16, name="qk_bf")
+            if t % PAIR == 0:
+                qk_of[(h, t // PAIR)] = per_pair.tile([PART, 2, PAIR, KEY_PITCH], BF16, name="qk_bf")
             picked_qk_of[(h, t)] = picks.tile([PART, 2, PIECE], F32, name="picked_qk")
             for a in range(2):
                 look_up(picked_qk_of[(h, t)][:, a, 0 : patches * PATCH], a * HEADS + h, t, patches)
 
         def round_queries_and_keys(h, t, patches):
             nc.vector.tensor_scalar(
-                out=qk_of[h][:, :, t : t + patches, 0:PATCH],
+                out=qk_of[(h, t // PAIR)][:, :, t % PAIR : t % PAIR + patches, 0:PATCH],
                 in0=picked_qk_of[(h, t)][:, :, 0 : patches * PATCH].rearrange("p a (t j) -> p a t j", t=patches),
                 scalar1=ROOT_SCALE,
                 scalar2=None,
                 op0=MULT,
             )
-            if t == 0:
+            if t % PAIR == 0:
+                u = t // PATCHES_PER_CLOUD
                 nc.vector.tensor_scalar(
-                    out=qk_of[h][:, 1, :, PATCH:KEYS].rearrange("p (u t) o -> p u (t o)", u=CLOUDS),
-                    in0=cq[:, h, :].unsqueeze(2).to_broadcast([PART, CLOUDS, PATCHES_PER_CLOUD]),
+                    out=qk_of[(h, t // PAIR)][:, 1, :, PATCH:KEYS].rearrange("p t o -> p (t o)"),
+                    in0=cq[:, h, u : u + 1].to_broadcast([PART, PAIR]),
                     scalar1=ROOT_SCALE,
                     scalar2=None,
                     op0=MULT,
@@ -255,8 +260,8 @@ def tile_serializedattention_b_kernel(tc, feat, cls_tok, wqkv, bqkv, wproj, bpro
                 e_ps = logit_banks.tile([PART, KEYS], F32, name="e_ps")
                 nc.tensor.matmul(
                     e_ps[:],
-                    lhsT=qk_of[h][:, 0, t, jb * PART : (jb + 1) * PART],
-                    rhs=qk_of[h][:, 1, t, 0:KEYS],
+                    lhsT=qk_of[(h, t // PAIR)][:, 0, t % PAIR, jb * PART : (jb + 1) * PART],
+                    rhs=qk_of[(h, t // PAIR)][:, 1, t % PAIR, 0:KEYS],
                     start=True,
                     stop=True,
                 )
@@ -331,7 +336,7 @@ def tile_serializedattention_b_kernel(tc, feat, cls_tok, wqkv, bqkv, wproj, bpro
             u = t // PATCHES_PER_CLOUD
             pair, place = divmod(i, PAIR)
             if place == 0:
-                att_ps_of[pair] = att_banks.tile([PART, PIECE], F32, name="att_ps")
+                att_ps_of[pair] = sums.tile([PART, PIECE], F32, name="att_ps", tag="sum_ps")
             att_ps = att_ps_of[pair]
             for ib in range(HALVES):
                 nc.tensor.matmul(
@@ -353,17 +358,24 @@ def tile_serializedattention_b_kernel(tc, feat, cls_tok, wqkv, bqkv, wproj, bpro
             h, g = pieces[pair]
             nc.scalar.copy(att_bf[:, h, g * PIECE : (g + 1) * PIECE], att_ps_of[pair][:])
 
-        def project_out(n, m):
-            cols = slice(n * CHUNK, (n + 1) * CHUNK)
-            out_ps = sums.tile([PART, CHUNK], F32, name="out_ps", tag="sum_ps")
-            for h in range(HEADS):
+        def add_up_out(n, m, heads):
+            if heads[0] == 0:
+                if n < CHUNKS - 1:
+                    out_ps_of[(n, m)] = sums.tile([PART, CHUNK], F32, name="out_ps", tag="sum_ps")
+                else:
+                    out_ps_of[(n, m)] = logit_banks.tile([PART, CHUNK], F32, name="out_ps", tag="e_ps")
+            for h in heads:
                 nc.tensor.matmul(
-                    out_ps[:],
+                    out_ps_of[(n, m)][:],
                     lhsT=wproj_sb[:, h, m * PART : (m + 1) * PART],
-                    rhs=att_bf[:, h, cols],
+                    rhs=att_bf[:, h, n * CHUNK : (n + 1) * CHUNK],
                     start=(h == 0),
                     stop=(h == HEADS - 1),
                 )
+
+        def store_out(n, m):
+            cols = slice(n * CHUNK, (n + 1) * CHUNK)
+            out_ps = out_ps_of[(n, m)]
             out_sb = results.tile([PART, CHUNK], F32, name="out_sb")
             bproj_m = bias[:, ROW_BLOCKS + m : ROW_BLOCKS + m + 1]
             if m % 2 == 0:
@@ -390,7 +402,7 @@ def tile_serializedattention_b_kernel(tc, feat, cls_tok, wqkv, bqkv, wproj, bpro
         out_blocks_of = {}
         for n in range(CHUNKS):
             for m in range(C_BLOCKS):
-                tick = PAIR * pieces.index((HEADS - 1, n)) + PAIR - 1 + 5 + m // 2
+                tick = PAIR * pieces.index((HEADS - 1, n)) + PAIR - 1 + 6 + m // 2
                 out_blocks_of.setdefault(tick, []).append((n, m))
         for tick in range(max(out_blocks_of) + 1):
             if 1 <= tick < HEADS:
@@ -405,12 +417,16 @@ def tile_serializedattention_b_kernel(tc, feat, cls_tok, wqkv, bqkv, wproj, bpro
                 divide(tick - 2)
             if 0 <= tick - 3 < UNITS:
                 copy_flipped(tick - 3)
-            if 0 <= tick - 4 < UNITS and (tick - 4) % PAIR == PAIR - 1:
-                copy_weighted_sums((tick - 4) // PAIR)
-            for r, n in projections[early + (3 * tick + 1) // 4 : early + (3 * tick + 4) // 4]:
+            if 0 <= tick - 5 < UNITS and (tick - 5) % PAIR == PAIR - 1:
+                copy_weighted_sums((tick - 5) // PAIR)
+            for r, n in projections[early + PACE * tick // 16 : early + PACE * (tick + 1) // 16]:
                 project_two_chunks(r, n)
+            if tick == UNITS:
+                for m in range(C_BLOCKS):
+                    add_up_out(CHUNKS - 1, m, range(HEADS - 1))
             for n, m in out_blocks_of.get(tick, []):
-                project_out(n, m)
+                add_up_out(n, m, range(HEADS) if n < CHUNKS - 1 else range(HEADS - 1, HEADS))
+                store_out(n, m)
             piece = tick // 2
             if tick % 2 == 0 and piece + 1 < HEADS * PIECES:
                 h, g = pieces[piece + 1]
@@ -426,5 +442,5 @@ def tile_serializedattention_b_kernel(tc, feat, cls_tok, wqkv, bqkv, wproj, bpro
                 reciprocals(tick - 1)
             if 0 <= tick - 2 < UNITS:
                 flip(tick - 2)
-            if 0 <= tick - 3 < UNITS:
-                weighted_sums(tick - 3)
+            if 0 <= tick - 4 < UNITS:
+                weighted_sums(tick - 4)

@@ -386,11 +386,11 @@ def tile_serializedattention_b_kernel(tc, feat, cls_tok, wqkv, bqkv, wproj, bpro
 
         for s in range(SLICES):
             round_slice(s)
-            if s % 2 == 0:
-                for r in row_order[3 * s // 2 : 3 * s // 2 + 3]:
-                    spread_bias(r)
-            for r in row_order[0:2]:
-                project_slice(r, s)
+            project_slice(row_order[0], s)
+        for s in range(SLICES):
+            project_slice(row_order[1], s)
+        for r in row_order:
+            spread_bias(r)
         class_tokens(0)
         for t in range(PAIR):
             look_up_queries_and_keys(0, t, 1)
@@ -409,38 +409,38 @@ def tile_serializedattention_b_kernel(tc, feat, cls_tok, wqkv, bqkv, wproj, bpro
                 class_tokens(tick)
             if 0 <= tick - 1 < HEADS:
                 class_value_rows(tick - 1)
+            piece = tick // 2
             if tick < UNITS:
                 logits(tick)
             if 0 <= tick - 1 < UNITS:
                 exponentials(tick - 1)
-            if 0 <= tick - 2 < UNITS:
-                divide(tick - 2)
             if 0 <= tick - 3 < UNITS:
                 copy_flipped(tick - 3)
-            if 0 <= tick - 5 < UNITS and (tick - 5) % PAIR == PAIR - 1:
-                copy_weighted_sums((tick - 5) // PAIR)
-            for r, n in projections[early + PACE * tick // 16 : early + PACE * (tick + 1) // 16]:
-                project_two_chunks(r, n)
-            if tick == UNITS:
+            if 0 <= tick - 2 < UNITS:
+                divide(tick - 2)
+            if 0 <= tick - 1 < UNITS:
+                reciprocals(tick - 1)
+            if 0 <= tick - 2 < UNITS:
+                flip(tick - 2)
+            if tick % 2 == 1 and piece + 1 < len(pieces):
+                h, g = pieces[piece + 1]
+                round_queries_and_keys(h, g * PAIR, PAIR)
+            if tick < UNITS:
+                maxima(tick)
+            if tick % 2 == 0 and piece + 1 < len(pieces):
+                h, g = pieces[piece + 1]
+                look_up_queries_and_keys(h, g * PAIR, PAIR)
+            if tick == UNITS + 1:
                 for m in range(C_BLOCKS):
                     add_up_out(CHUNKS - 1, m, range(HEADS - 1))
             for n, m in out_blocks_of.get(tick, []):
                 add_up_out(n, m, range(HEADS) if n < CHUNKS - 1 else range(HEADS - 1, HEADS))
                 store_out(n, m)
-            piece = tick // 2
-            if tick % 2 == 0 and piece + 1 < HEADS * PIECES:
-                h, g = pieces[piece + 1]
-                look_up_queries_and_keys(h, g * PAIR, PAIR)
-            if tick % 2 == 1 and piece + 1 < HEADS * PIECES:
-                h, g = pieces[piece + 1]
-                round_queries_and_keys(h, g * PAIR, PAIR)
-            if tick % 2 == 1 and piece < HEADS * PIECES:
+            if 0 <= tick - 5 < UNITS and (tick - 5) % PAIR == PAIR - 1:
+                copy_weighted_sums((tick - 5) // PAIR)
+            if tick % 2 == 1 and piece < len(pieces):
                 look_up_values(*pieces[piece])
-            if tick < UNITS:
-                maxima(tick)
-            if 0 <= tick - 1 < UNITS:
-                reciprocals(tick - 1)
-            if 0 <= tick - 2 < UNITS:
-                flip(tick - 2)
+            for r, n in projections[early + PACE * tick // 16 : early + PACE * (tick + 1) // 16]:
+                project_two_chunks(r, n)
             if 0 <= tick - 4 < UNITS:
                 weighted_sums(tick - 4)

@@ -236,16 +236,12 @@ def tile_serializedattention_b_kernel(tc, feat, cls_tok, wqkv, bqkv, wproj, bpro
                         start=(cb == 0),
                         stop=(cb == C_BLOCKS - 1),
                     )
-            nc.vector.tensor_tensor(
-                cq[:].rearrange("p (k h) u -> p k h u", k=2)[:, :, h, :],
-                cq_ps[:],
-                bias[:, HEADS:ROW_BLOCKS]
-                .rearrange("p (k h) -> p k h", k=2)[:, :, h]
-                .unsqueeze(2)
-                .to_broadcast([PART, 2, CLOUDS]),
-                ADD,
-            )
-            nc.vector.tensor_copy(cv_spread[:, h, :, :], cq[:, HEADS + h, :].unsqueeze(2).to_broadcast([PART, CLOUDS, PART]))
+            for kind in range(2):
+                r = (1 + kind) * HEADS + h
+                nc.scalar.activation(
+                    out=cq[:, kind * HEADS + h, :], in_=cq_ps[:, kind, :], func=IDENTITY, bias=bias[:, r : r + 1]
+                )
+            nc.scalar.copy(cv_spread[:, h, :, :], cq[:, HEADS + h, :].unsqueeze(2).to_broadcast([PART, CLOUDS, PART]))
 
         def class_value_rows(h):
             cv_ps = sums.tile([PART, CLOUDS, DH], F32, name="cv_ps", tag="sum_ps")
@@ -291,22 +287,23 @@ def tile_serializedattention_b_kernel(tc, feat, cls_tok, wqkv, bqkv, wproj, bpro
         def reciprocals(i):
             recip_of[i] = stats.tile([PART, HALVES], F32, name="recip")
             nc.vector.reciprocal(recip_of[i][:], total_of[i][:])
+
+        def divide(i):
+            w_of[i] = per_unit.tile([PART, HALVES, KEY_PITCH], BF16, name="w")
+            for jb in range(HALVES):
+                nc.scalar.activation(
+                    out=w_of[i][:, jb, 0:KEYS], in_=ex_of[i][jb][:], func=COPY, scale=recip_of[i][:, jb : jb + 1]
+                )
+
+        def diagonals_of_class_weights(i):
             diag_of[i] = diagonals.tile([PART, HALVES, PART], BF16, name="diag")
             for jb in range(HALVES):
                 nc.vector.tensor_scalar(
                     out=diag_of[i][:, jb, :],
                     in0=ident[:],
-                    scalar1=ex_of[i][jb][:, PATCH:KEYS],
-                    scalar2=recip_of[i][:, jb : jb + 1],
+                    scalar1=w_of[i][:, jb, PATCH:KEYS],
+                    scalar2=None,
                     op0=MULT,
-                    op1=MULT,
-                )
-
-        def divide(i):
-            w_of[i] = per_unit.tile([PART, HALVES, PATCH], BF16, name="w")
-            for jb in range(HALVES):
-                nc.scalar.activation(
-                    out=w_of[i][:, jb, :], in_=ex_of[i][jb][:, 0:PATCH], func=COPY, scale=recip_of[i][:, jb : jb + 1]
                 )
 
         def flip(i):
@@ -398,6 +395,10 @@ def tile_serializedattention_b_kernel(tc, feat, cls_tok, wqkv, bqkv, wproj, bpro
         early = 2
         for r, n in projections[0:early]:
             project_two_chunks(r, n)
+        for h in range(1, HEADS):
+            class_tokens(h)
+        for h in range(HEADS):
+            class_value_rows(h)
 
         out_blocks_of = {}
         for n in range(CHUNKS):
@@ -405,10 +406,6 @@ def tile_serializedattention_b_kernel(tc, feat, cls_tok, wqkv, bqkv, wproj, bpro
                 tick = PAIR * pieces.index((HEADS - 1, n)) + PAIR - 1 + 6 + m // 2
                 out_blocks_of.setdefault(tick, []).append((n, m))
         for tick in range(max(out_blocks_of) + 1):
-            if 1 <= tick < HEADS:
-                class_tokens(tick)
-            if 0 <= tick - 1 < HEADS:
-                class_value_rows(tick - 1)
             piece = tick // 2
             if tick < UNITS:
                 logits(tick)
@@ -442,5 +439,7 @@ def tile_serializedattention_b_kernel(tc, feat, cls_tok, wqkv, bqkv, wproj, bpro
                 look_up_values(*pieces[piece])
             for r, n in projections[early + PACE * tick // 16 : early + PACE * (tick + 1) // 16]:
                 project_two_chunks(r, n)
+            if 0 <= tick - 3 < UNITS:
+                diagonals_of_class_weights(tick - 3)
             if 0 <= tick - 4 < UNITS:
                 weighted_sums(tick - 4)

@@ -59,7 +59,7 @@ def tile_serializedattention_b_kernel(tc, feat, cls_tok, wqkv, bqkv, wproj, bpro
         exps = ctx.enter_context(tc.tile_pool(name="exps", bufs=8))
         per_unit = ctx.enter_context(tc.tile_pool(name="per_unit", bufs=6))
         diagonals = ctx.enter_context(tc.tile_pool(name="diagonals", bufs=6))
-        results = ctx.enter_context(tc.tile_pool(name="results", bufs=4))
+        results = ctx.enter_context(tc.tile_pool(name="results", bufs=8))
         sums = ctx.enter_context(tc.psum_pool(name="sums", bufs=3))
         logit_banks = ctx.enter_context(tc.psum_pool(name="logit_banks", bufs=4))
         flips = ctx.enter_context(tc.psum_pool(name="flips", bufs=1))

@@ -389,9 +389,8 @@ def tile_serializedattention_b_kernel(tc, feat, cls_tok, wqkv, bqkv, wproj, bpro
         for r in row_order:
             spread_bias(r)
         class_tokens(0)
-        for t in range(PAIR):
-            look_up_queries_and_keys(0, t, 1)
-            round_queries_and_keys(0, t, 1)
+        look_up_queries_and_keys(0, 0, PAIR)
+        round_queries_and_keys(0, 0, PAIR)
         early = 2
         for r, n in projections[0:early]:
             project_two_chunks(r, n)

@@ -30,7 +30,8 @@ ROW_BLOCKS = 3 * C // PART
 CHUNK = 512
 CHUNKS = POINTS // CHUNK
 SLICE = CHUNK // 2
-SLICES = POINTS // SLICE
+FIRST_COLUMNS = [0, SLICE // 2] + list(range(SLICE, POINTS, SLICE)) + [POINTS - SLICE // 2]
+SLICES = [slice(a, b) for a, b in zip(FIRST_COLUMNS, FIRST_COLUMNS[1:] + [POINTS])]
 HALVES = PATCH // PART
 PAIR = 2
 PIECE = PAIR * PATCH
@@ -75,19 +76,17 @@ def tile_serializedattention_b_kernel(tc, feat, cls_tok, wqkv, bqkv, wproj, bpro
         nc.vector.memset(bias_rows[:], 0.0)
         staged_of = {}
 
-        def load_slice(s):
-            n, half = divmod(s, CHUNK // SLICE)
-            if half == 0:
+        def staged(cols):
+            n, first = divmod(cols.start, CHUNK)
+            if n not in staged_of:
                 staged_of[n] = windows.tile([PART, C_BLOCKS, CHUNK], F32, name="staged", tag="window")
-            nc.sync.dma_start(
-                staged_of[n][:, :, half * SLICE : (half + 1) * SLICE], feat_blocks[:, :, s * SLICE : (s + 1) * SLICE]
-            )
+            return staged_of[n][:, :, first : first + cols.stop - cols.start]
 
-        def round_slice(s):
-            n, half = divmod(s, CHUNK // SLICE)
-            nc.vector.tensor_copy(
-                feat_bf[:, :, s * SLICE : (s + 1) * SLICE], staged_of[n][:, :, half * SLICE : (half + 1) * SLICE]
-            )
+        def load_slice(cols):
+            nc.sync.dma_start(staged(cols), feat_blocks[:, :, cols])
+
+        def round_slice(cols):
+            nc.vector.tensor_copy(feat_bf[:, :, cols], staged(cols))
 
         def load_wqkv(kind, first_head, heads):
             cols = slice(kind * C + first_head * DH, kind * C + (first_head + heads) * DH)
@@ -99,10 +98,11 @@ def tile_serializedattention_b_kernel(tc, feat, cls_tok, wqkv, bqkv, wproj, bpro
         )
         nc.scalar.dma_start(cls_sb[:], cls_tok.rearrange("(cb p) u -> p cb u", p=PART))
         load_wqkv(0, 0, 1)
+        load_slice(SLICES[0])
         load_wqkv(1, 0, 1)
+        for cols in SLICES[1:]:
+            load_slice(cols)
         nc.sync.dma_start(offsets[:], offs)
-        for s in range(SLICES):
-            load_slice(s)
         load_wqkv(2, 0, 1)
         for kind in range(3):
             load_wqkv(kind, 1, HEADS - 1)
@@ -118,8 +118,8 @@ def tile_serializedattention_b_kernel(tc, feat, cls_tok, wqkv, bqkv, wproj, bpro
         ident = held.tile([PART, PART], BF16, name="ident")
         make_identity(nc, ident[:])
 
-        bias_ps = sums.tile([PART, CHUNK], F32, name="bias_ps", tag="sum_ps")
-        nc.tensor.transpose(bias_ps[:, 0:PART], bias_rows[:], ident_f32[:])
+        bias_ps = flips.tile([PART, PART], F32, name="bias_ps", tag="flip_ps")
+        nc.tensor.transpose(bias_ps[:], bias_rows[:], ident_f32[:])
         bias = held.tile([PART, ROW_BLOCKS + C_BLOCKS], F32, name="bias")
         nc.vector.tensor_copy(bias[:], bias_ps[:, 0 : ROW_BLOCKS + C_BLOCKS])
         bias_wide = held.tile([PART, ROW_BLOCKS, PIECE], F32, name="bias_wide")
@@ -148,14 +148,14 @@ def tile_serializedattention_b_kernel(tc, feat, cls_tok, wqkv, bqkv, wproj, bpro
         out_ps_of = {}
         att_ps_of = {}
 
-        def project_slice(r, s):
-            if s == 0:
+        def project_slice(r, cols):
+            width = cols.stop - cols.start
+            if cols.start == 0:
                 window_of[r] = windows.tile([PART, POINTS], F32, name="window")
-            cols = slice(s * SLICE, (s + 1) * SLICE)
             if r < HEADS:
-                p_ps = sums.tile([PART, SLICE], F32, name="p_ps", tag="sum_ps")
+                p_ps = sums.tile([PART, width], F32, name="p_ps", tag="sum_ps")
             else:
-                p_ps = logit_banks.tile([PART, SLICE], F32, name="p_ps", tag="e_ps")
+                p_ps = logit_banks.tile([PART, width], F32, name="p_ps", tag="e_ps")
             for cb in range(C_BLOCKS):
                 nc.tensor.matmul(
                     p_ps[:],
@@ -381,11 +381,11 @@ def tile_serializedattention_b_kernel(tc, feat, cls_tok, wqkv, bqkv, wproj, bpro
                 nc.vector.tensor_scalar(out=out_sb[:], in0=out_ps[:], scalar1=bproj_m, scalar2=None, op0=ADD)
             nc.sync.dma_start(out[m * PART : (m + 1) * PART, cols], out_sb[:])
 
-        for s in range(SLICES):
-            round_slice(s)
-            project_slice(row_order[0], s)
-        for s in range(SLICES):
-            project_slice(row_order[1], s)
+        for cols in SLICES:
+            round_slice(cols)
+            project_slice(row_order[0], cols)
+        for cols in SLICES:
+            project_slice(row_order[1], cols)
         for r in row_order:
             spread_bias(r)
         class_tokens(0)

from contextlib import ExitStack

import concourse.mybir as mybir
from concourse.masks import make_identity

F32 = mybir.dt.float32
BF16 = mybir.dt.bfloat16
U16 = mybir.dt.uint16
ADD = mybir.AluOpType.add
MULT = mybir.AluOpType.mult
EXP = mybir.ActivationFunctionType.Exp
IDENTITY = mybir.ActivationFunctionType.Identity
COPY = mybir.ActivationFunctionType.Copy
ALONG_FREE = mybir.AxisListType.X

PART = 128
C = 512
POINTS = 2048
HEADS = 4
DH = C // HEADS
PATCH = 256
PATCHES = POINTS // PATCH
UNITS = HEADS * PATCHES
CLOUDS = 2
PATCHES_PER_CLOUD = PATCHES // CLOUDS
KEYS = PATCH + 1
KEY_PITCH = 264
C_BLOCKS = C // PART
ROW_BLOCKS = 3 * C // PART
CHUNK = 512
CHUNKS = POINTS // CHUNK
SLICE = CHUNK // 2
FIRST_COLUMNS = [0, SLICE // 2] + list(range(SLICE, POINTS, SLICE)) + [POINTS - SLICE // 2]
SLICES = [slice(a, b) for a, b in zip(FIRST_COLUMNS, FIRST_COLUMNS[1:] + [POINTS])]
HALVES = PATCH // PART
PAIR = 2
PIECE = PAIR * PATCH
PIECES = POINTS // PIECE
OFFSET_COLS = PATCH // 16
PACE = 15
ROOT_SCALE = DH**-0.25

FLOPS = (
    2 * C * 3 * C * POINTS
    + 2 * C * 2 * C * CLOUDS
    + 2 * 2 * HEADS * PATCHES * DH * PATCH * KEYS
    + 2 * C * C * POINTS
)


def tile_serializedattention_b_kernel(tc, feat, cls_tok, wqkv, bqkv, wproj, bproj, offs, out):
    nc = tc.nc
    with ExitStack() as ctx:
        held = ctx.enter_context(tc.tile_pool(name="held", bufs=1))
        windows = ctx.enter_context(tc.tile_pool(name="windows", bufs=8))
        picks = ctx.enter_context(tc.tile_pool(name="picks", bufs=1))
        per_head = ctx.enter_context(tc.tile_pool(name="per_head", bufs=2))
        per_pair = ctx.enter_context(tc.tile_pool(name="per_pair", bufs=1))
        stats = ctx.enter_context(tc.tile_pool(name="stats", bufs=12))
        exps = ctx.enter_context(tc.tile_pool(name="exps", bufs=8))
        per_unit = ctx.enter_context(tc.tile_pool(name="per_unit", bufs=6))
        diagonals = ctx.enter_context(tc.tile_pool(name="diagonals", bufs=6))
        results = ctx.enter_context(tc.tile_pool(name="results", bufs=8))
        sums = ctx.enter_context(tc.psum_pool(name="sums", bufs=3))
        logit_banks = ctx.enter_context(tc.psum_pool(name="logit_banks", bufs=4))
        flips = ctx.enter_context(tc.psum_pool(name="flips", bufs=1))

        offsets = held.tile([PART, POINTS // 16], U16, name="offsets")
        wqkv_sb = held.tile([PART, C_BLOCKS, 3 * C], BF16, name="wqkv_sb")
        wqkv_blocks = wqkv.rearrange("(cb p) r -> p cb r", p=PART)
        wproj_sb = held.tile([PART, C_BLOCKS, C], BF16, name="wproj_sb")
        feat_bf = held.tile([PART, C_BLOCKS, POINTS], BF16, name="feat_bf")
        feat_blocks = feat.rearrange("(cb p) s -> p cb s", p=PART)
        cls_sb = held.tile([PART, C_BLOCKS, CLOUDS], BF16, name="cls_sb")
        bias_rows = held.tile([PART, PART], F32, name="bias_rows")
        nc.vector.memset(bias_rows[:], 0.0)
        staged_of = {}

        def staged(cols):
            n, first = divmod(cols.start, CHUNK)
            if n not in staged_of:
                staged_of[n] = windows.tile([PART, C_BLOCKS, CHUNK], F32, name="staged", tag="window")
            return staged_of[n][:, :, first : first + cols.stop - cols.start]

        def load_slice(cols):
            nc.sync.dma_start(staged(cols), feat_blocks[:, :, cols])

        def round_slice(cols):
            nc.vector.tensor_copy(feat_bf[:, :, cols], staged(cols))

        def load_wqkv(kind, first_head, heads):
            cols = slice(kind * C + first_head * DH, kind * C + (first_head + heads) * DH)
            nc.sync.dma_start(wqkv_sb[:, :, cols], wqkv_blocks[:, :, cols])

        nc.scalar.dma_start(bias_rows[0:ROW_BLOCKS, :], bqkv.rearrange("(b p) o -> b (p o)", p=PART))
        nc.scalar.dma_start(
            bias_rows[ROW_BLOCKS : ROW_BLOCKS + C_BLOCKS, :], bproj.rearrange("(b p) o -> b (p o)", p=PART)
        )
        nc.scalar.dma_start(cls_sb[:], cls_tok.rearrange("(cb p) u -> p cb u", p=PART))
        load_wqkv(0, 0, 1)
        load_slice(SLICES[0])
        load_wqkv(1, 0, 1)
        for cols in SLICES[1:]:
            load_slice(cols)
        nc.sync.dma_start(offsets[:], offs)
        load_wqkv(2, 0, 1)
        for kind in range(3):
            load_wqkv(kind, 1, HEADS - 1)
        nc.sync.dma_start(wproj_sb[:], wproj.rearrange("(cb p) m -> p cb m", p=PART))

        zero = held.tile([PART, 1], F32, name="zero")
        nc.vector.memset(zero[:], 0.0)
        one = held.tile([PART, 1], F32, name="one")
        nc.scalar.activation(out=one[:], in_=zero[:], func=EXP)

        ident_f32 = held.tile([PART, PART], F32, name="ident_f32")
        make_identity(nc, ident_f32[:])
        ident = held.tile([PART, PART], BF16, name="ident")
        make_identity(nc, ident[:])

        bias_ps = flips.tile([PART, PART], F32, name="bias_ps", tag="flip_ps")
        nc.tensor.transpose(bias_ps[:], bias_rows[:], ident_f32[:])
        bias = held.tile([PART, ROW_BLOCKS + C_BLOCKS], F32, name="bias")
        nc.vector.tensor_copy(bias[:], bias_ps[:, 0 : ROW_BLOCKS + C_BLOCKS])
        bias_wide = held.tile([PART, ROW_BLOCKS, PIECE], F32, name="bias_wide")

        def spread_bias(r):
            nc.vector.tensor_copy(bias_wide[:, r, :], bias[:, r : r + 1].to_broadcast([PART, PIECE]))

        begins = (0, PIECES, 2 * PIECES, 2 * PIECES + 1)
        pieces = sorted([(h, g) for h in range(HEADS) for g in range(PIECES)], key=lambda hg: begins[hg[0]] + hg[1])
        units = [(h, PAIR * g + k) for h, g in pieces for k in range(PAIR)]
        row_order = [r for h in range(HEADS) for r in (h, HEADS + h, 2 * HEADS + h)]
        projections = [(r, n) for r in row_order[2:] for n in range(0, CHUNKS, 2)]

        cq = held.tile([PART, 2 * HEADS, CLOUDS], F32, name="cq")
        cv_spread = held.tile([PART, HEADS, CLOUDS, PART], BF16, name="cv_spread")
        cv_rows = held.tile([PART, HEADS, CLOUDS, DH], BF16, name="cv_rows")
        att_bf = held.tile([PART, HEADS, POINTS], BF16, name="att_bf")

        window_of = {}
        picked_qk_of = {}
        qk_of = {}
        v_of = {}
        e_of, shift_of, ex_of, total_of, recip_of = {}, {}, {}, {}, {}
        w_of, diag_of = {}, {}
        flip_ps_of, flipped_of = {}, {}
        out_ps_of = {}
        att_ps_of = {}

        def project_slice(r, cols):
            width = cols.stop - cols.start
            if cols.start == 0:
                window_of[r] = windows.tile([PART, POINTS], F32, name="window")
            if r < HEADS:
                p_ps = sums.tile([PART, width], F32, name="p_ps", tag="sum_ps")
            else:
                p_ps = logit_banks.tile([PART, width], F32, name="p_ps", tag="e_ps")
            for cb in range(C_BLOCKS):
                nc.tensor.matmul(
                    p_ps[:],
                    lhsT=wqkv_sb[:, cb, r * PART : (r + 1) * PART],
                    rhs=feat_bf[:, cb, cols],
                    start=(cb == 0),
                    stop=(cb == C_BLOCKS - 1),
                )
            nc.scalar.copy(window_of[r][:, cols], p_ps[:])

        def project_two_chunks(r, first):
            if first == 0:
                window_of[r] = windows.tile([PART, POINTS], F32, name="window")
            banks = [sums.tile([PART, CHUNK], F32, name="p_ps", tag="sum_ps") for n in range(2)]
            for cb in range(C_BLOCKS):
                for i in range(2):
                    n = first + i
                    nc.tensor.matmul(
                        banks[i][:],
                        lhsT=wqkv_sb[:, cb, r * PART : (r + 1) * PART],
                        rhs=feat_bf[:, cb, n * CHUNK : (n + 1) * CHUNK],
                        start=(cb == 0),
                        stop=(cb == C_BLOCKS - 1),
                    )
            for i in range(2):
                n = first + i
                nc.scalar.copy(window_of[r][:, n * CHUNK : (n + 1) * CHUNK], banks[i][:])

        def look_up(dest, r, t, patches):
            nc.vector.tensor_tensor(
                dest,
                window_of[r][:].indirect(offsets[:, t * OFFSET_COLS : (t + patches) * OFFSET_COLS]),
                bias_wide[:, r, 0 : patches * PATCH],
                ADD,
            )

        def look_up_queries_and_keys(h, t, patches):
            if t % PAIR == 0:
                qk_of[(h, t // PAIR)] = per_pair.tile([PART, 2, PAIR, KEY_PITCH], BF16, name="qk_bf")
            picked_qk_of[(h, t)] = picks.tile([PART, 2, PIECE], F32, name="picked_qk")
            for a in range(2):
                look_up(picked_qk_of[(h, t)][:, a, 0 : patches * PATCH], a * HEADS + h, t, patches)

        def round_queries_and_keys(h, t, patches):
            nc.vector.tensor_scalar(
                out=qk_of[(h, t // PAIR)][:, :, t % PAIR : t % PAIR + patches, 0:PATCH],
                in0=picked_qk_of[(h, t)][:, :, 0 : patches * PATCH].rearrange("p a (t j) -> p a t j", t=patches),
                scalar1=ROOT_SCALE,
                scalar2=None,
                op0=MULT,
            )
            if t % PAIR == 0:
                u = t // PATCHES_PER_CLOUD
                nc.vector.tensor_scalar(
                    out=qk_of[(h, t // PAIR)][:, 1, :, PATCH:KEYS].rearrange("p t o -> p (t o)"),
                    in0=cq[:, h, u : u + 1].to_broadcast([PART, PAIR]),
                    scalar1=ROOT_SCALE,
                    scalar2=None,
                    op0=MULT,
                )

        def look_up_values(h, g):
            if g == 0:
                v_of[h] = per_head.tile([PART, POINTS], BF16, name="v_bf")
            picked_v = picks.tile([PART, PIECE], F32, name="picked_v")
            look_up(picked_v[:], 2 * HEADS + h, g * PAIR, PAIR)
            nc.scalar.copy(v_of[h][:, g * PIECE : (g + 1) * PIECE], picked_v[:])

        def class_tokens(h):
            cq_ps = sums.tile([PART, 2, CLOUDS], F32, name="cq_ps", tag="sum_ps")
            for kind in range(2):
                r = (1 + kind) * HEADS + h
                for cb in range(C_BLOCKS):
                    nc.tensor.matmul(
                        cq_ps[:, kind, :],
                        lhsT=wqkv_sb[:, cb, r * PART : (r + 1) * PART],
                        rhs=cls_sb[:, cb, :],
                        start=(cb == 0),
                        stop=(cb == C_BLOCKS - 1),
                    )
            for kind in range(2):
                r = (1 + kind) * HEADS + h
                nc.scalar.activation(
                    out=cq[:, kind * HEADS + h, :], in_=cq_ps[:, kind, :], func=IDENTITY, bias=bias[:, r : r + 1]
                )
            nc.scalar.copy(cv_spread[:, h, :, :], cq[:, HEADS + h, :].unsqueeze(2).to_broadcast([PART, CLOUDS, PART]))

        def class_value_rows(h):
            cv_ps = sums.tile([PART, CLOUDS, DH], F32, name="cv_ps", tag="sum_ps")
            for u in range(CLOUDS):
                nc.tensor.matmul(cv_ps[:, u, :], lhsT=cv_spread[:, h, u, :], rhs=ident[:], start=True, stop=True)
            nc.scalar.copy(cv_rows[:, h, :, :], cv_ps[:])

        def logits(i):
            h, t = units[i]
            e_of[i] = []
            for jb in range(HALVES):
                e_ps = logit_banks.tile([PART, KEYS], F32, name="e_ps")
                nc.tensor.matmul(
                    e_ps[:],
                    lhsT=qk_of[(h, t // PAIR)][:, 0, t % PAIR, jb * PART : (jb + 1) * PART],
                    rhs=qk_of[(h, t // PAIR)][:, 1, t % PAIR, 0:KEYS],
                    start=True,
                    stop=True,
                )
                e_of[i].append(e_ps)

        def maxima(i):
            shift_of[i] = stats.tile([PART, HALVES], F32, name="shift")
            for jb in range(HALVES):
                nc.vector.reduce_max(
                    out=shift_of[i][:, jb : jb + 1], in_=e_of[i][jb][:], axis=ALONG_FREE, negate=True
                )

        def exponentials(i):
            total_of[i] = stats.tile([PART, HALVES], F32, name="total")
            ex_of[i] = []
            for jb in range(HALVES):
                ex = exps.tile([PART, KEYS], F32, name="ex")
                nc.scalar.activation(
                    out=ex[:],
                    in_=e_of[i][jb][:],
                    func=EXP,
                    bias=shift_of[i][:, jb : jb + 1],
                    accum_out=total_of[i][:, jb : jb + 1],
                )
                ex_of[i].append(ex)

        def reciprocals(i):
            recip_of[i] = stats.tile([PART, HALVES], F32, name="recip")
            nc.vector.reciprocal(recip_of[i][:], total_of[i][:])

        def divide(i):
            w_of[i] = per_unit.tile([PART, HALVES, KEY_PITCH], BF16, name="w")
            for jb in range(HALVES):
                nc.scalar.activation(
                    out=w_of[i][:, jb, 0:KEYS], in_=ex_of[i][jb][:], func=COPY, scale=recip_of[i][:, jb : jb + 1]
                )

        def diagonals_of_class_weights(i):
            diag_of[i] = diagonals.tile([PART, HALVES, PART], BF16, name="diag")
            for jb in range(HALVES):
                nc.vector.tensor_scalar(
                    out=diag_of[i][:, jb, :],
                    in0=ident[:],
                    scalar1=w_of[i][:, jb, PATCH:KEYS],
                    scalar2=None,
                    op0=MULT,
                )

        def flip(i):
            h, t = units[i]
            flip_ps = flips.tile([PART, HALVES * (PATCH + DH)], BF16, name="flip_ps")
            for ib in range(HALVES):
                for jb in range(HALVES):
                    nc.tensor.transpose(
                        flip_ps[:, ib * PATCH + jb * PART : ib * PATCH + (jb + 1) * PART],
                        w_of[i][:, jb, ib * PART : (ib + 1) * PART],
                        ident[:],
                    )
            for ib in range(HALVES):
                nc.tensor.transpose(
                    flip_ps[:, HALVES * PATCH + ib * DH : HALVES * PATCH + (ib + 1) * DH],
                    v_of[h][:, t * PATCH + ib * PART : t * PATCH + (ib + 1) * PART],
                    ident[:],
                )
            flip_ps_of[i] = flip_ps

        def copy_flipped(i):
            flipped_of[i] = per_unit.tile([PART, HALVES * (PATCH + DH)], BF16, name="flipped")
            nc.scalar.copy(flipped_of[i][:], flip_ps_of[i][:])

        def weighted_sums(i):
            h, t = units[i]
            u = t // PATCHES_PER_CLOUD
            pair, place = divmod(i, PAIR)
            if place == 0:
                att_ps_of[pair] = sums.tile([PART, PIECE], F32, name="att_ps", tag="sum_ps")
            att_ps = att_ps_of[pair]
            for ib in range(HALVES):
                nc.tensor.matmul(
                    att_ps[:, place * PATCH : (place + 1) * PATCH],
                    lhsT=flipped_of[i][:, HALVES * PATCH + ib * DH : HALVES * PATCH + (ib + 1) * DH],
                    rhs=flipped_of[i][:, ib * PATCH : (ib + 1) * PATCH],
                    start=(ib == 0),
                    stop=False,
                )
            nc.tensor.matmul(
                att_ps[:, place * PATCH : (place + 1) * PATCH],
                lhsT=cv_rows[:, h, u, :],
                rhs=diag_of[i][:].rearrange("p b j -> p (b j)"),
                start=False,
                stop=True,
            )

        def copy_weighted_sums(pair):
            h, g = pieces[pair]
            nc.scalar.copy(att_bf[:, h, g * PIECE : (g + 1) * PIECE], att_ps_of[pair][:])

        def add_up_out(n, m, heads):
            if heads[0] == 0:
                if n < CHUNKS - 1:
                    out_ps_of[(n, m)] = sums.tile([PART, CHUNK], F32, name="out_ps", tag="sum_ps")
                else:
                    out_ps_of[(n, m)] = logit_banks.tile([PART, CHUNK], F32, name="out_ps", tag="e_ps")
            for h in heads:
                nc.tensor.matmul(
                    out_ps_of[(n, m)][:],
                    lhsT=wproj_sb[:, h, m * PART : (m + 1) * PART],
                    rhs=att_bf[:, h, n * CHUNK : (n + 1) * CHUNK],
                    start=(h == 0),
                    stop=(h == HEADS - 1),
                )

        def store_out(n, m):
            cols = slice(n * CHUNK, (n + 1) * CHUNK)
            out_ps = out_ps_of[(n, m)]
            out_sb = results.tile([PART, CHUNK], F32, name="out_sb")
            bproj_m = bias[:, ROW_BLOCKS + m : ROW_BLOCKS + m + 1]
            if m % 2 == 0:
                nc.scalar.activation(out=out_sb[:], in_=out_ps[:], func=IDENTITY, bias=bproj_m)
            else:
                nc.vector.tensor_scalar(out=out_sb[:], in0=out_ps[:], scalar1=bproj_m, scalar2=None, op0=ADD)
            nc.sync.dma_start(out[m * PART : (m + 1) * PART, cols], out_sb[:])

        for cols in SLICES:
            round_slice(cols)
            project_slice(row_order[0], cols)
        for cols in SLICES:
            project_slice(row_order[1], cols)
        for r in row_order:
            spread_bias(r)
        class_tokens(0)
        look_up_queries_and_keys(0, 0, PAIR)
        round_queries_and_keys(0, 0, PAIR)
        early = 2
        for r, n in projections[0:early]:
            project_two_chunks(r, n)
        for h in range(1, HEADS):
            class_tokens(h)
        for h in range(HEADS):
            class_value_rows(h)

        out_blocks_of = {}
        for n in range(CHUNKS):
            for m in range(C_BLOCKS):
                tick = PAIR * pieces.index((HEADS - 1, n)) + PAIR - 1 + 6 + m // 2
                out_blocks_of.setdefault(tick, []).append((n, m))
        for tick in range(max(out_blocks_of) + 1):
            piece = tick // 2
            if tick < UNITS:
                logits(tick)
            if 0 <= tick - 1 < UNITS:
                exponentials(tick - 1)
            if 0 <= tick - 3 < UNITS:
                copy_flipped(tick - 3)
            if 0 <= tick - 2 < UNITS:
                divide(tick - 2)
            if 0 <= tick - 1 < UNITS:
                reciprocals(tick - 1)
            if 0 <= tick - 2 < UNITS:
                flip(tick - 2)
            if tick % 2 == 1 and piece + 1 < len(pieces):
                h, g = pieces[piece + 1]
                round_queries_and_keys(h, g * PAIR, PAIR)
            if tick < UNITS:
                maxima(tick)
            if tick % 2 == 0 and piece + 1 < len(pieces):
                h, g = pieces[piece + 1]
                look_up_queries_and_keys(h, g * PAIR, PAIR)
            if tick == UNITS + 1:
                for m in range(C_BLOCKS):
                    add_up_out(CHUNKS - 1, m, range(HEADS - 1))
            for n, m in out_blocks_of.get(tick, []):
                add_up_out(n, m, range(HEADS) if n < CHUNKS - 1 else range(HEADS - 1, HEADS))
                store_out(n, m)
            if 0 <= tick - 5 < UNITS and (tick - 5) % PAIR == PAIR - 1:
                copy_weighted_sums((tick - 5) // PAIR)
            if tick % 2 == 1 and piece < len(pieces):
                look_up_values(*pieces[piece])
            for r, n in projections[early + PACE * tick // 16 : early + PACE * (tick + 1) // 16]:
                project_two_chunks(r, n)
            if 0 <= tick - 3 < UNITS:
                diagonals_of_class_weights(tick - 3)
            if 0 <= tick - 4 < UNITS:
                weighted_sums(tick - 4)
